import numpy as np
import ml_dtypes


def mxq(x, axis, fmt="e4m3"):
    dtype, down = {"e4m3": (ml_dtypes.float8_e4m3fn, 7), "e5m2": (ml_dtypes.float8_e5m2, 14)}[fmt]
    v = np.moveaxis(np.asarray(x, np.float32).astype(ml_dtypes.bfloat16).astype(np.float64), axis, -1)
    blocks = v.reshape(v.shape[:-1] + (-1, 32))
    amax = np.abs(blocks).max(-1, keepdims=True)
    byte = np.maximum(np.where(amax > 0, np.frexp(amax)[1] - 1 + 127, 0) - down, 1)
    scale = np.exp2(byte - 127.0)
    codes = (blocks / scale).astype(np.float32).astype(dtype).astype(np.float64)
    return np.moveaxis((codes * scale).reshape(v.shape), -1, axis)


WIDE = False


def mx_kscale(k):
    if not WIDE:
        return np.ones(k)
    levels = np.array([10, -10, 5, -5, 0])
    a = np.random.permutation(np.resize(levels, k // 512 * 4)).reshape(k // 512, 4)
    idx = np.arange(k)
    return np.exp2(a[idx // 512, idx % 128 // 32])


BF16 = ml_dtypes.bfloat16


def bf(x):
    return np.asarray(x, np.float32).astype(BF16)


def f64(x):
    return np.asarray(x).astype(np.float64)


B, K, D, H1, H2, C = 4096, 2, 1024, 512, 128, 64


def setup_inputs():
    s, t = mx_kscale(D), mx_kscale(H1)
    return {"nf0": bf(np.random.standard_normal((B, D)) * s),
            "nf1": bf(np.random.standard_normal((B * K, D)) * s),
            "a1": bf(np.maximum(np.random.standard_normal((B * K, H1)) * np.sqrt(1.0 + 1.0 / K), 0.0) * t),
            "w1_0": bf(np.random.standard_normal((D, H1)) / np.sqrt(D) / s[:, None] * t),
            "w2_0": bf(np.random.standard_normal((D, H1)) / np.sqrt(D) / s[:, None] * t),
            "w1_1": bf(np.random.standard_normal((H1, H2)) / np.sqrt(H1) / t[:, None]),
            "w2_1": bf(np.random.standard_normal((H1, H2)) / np.sqrt(H1) / t[:, None])}


def sage_gcn(cur, neigh, w1, w2):
    b, d = cur.shape
    agg = neigh.reshape(b, -1, d).mean(axis=1)
    return np.maximum((mxq(cur, 1, "e4m3") @ mxq(w2, 0, "e4m3")) + (mxq(agg, 1, "e4m3") @ mxq(w1, 0, "e4m3")), 0.0)


def reference(nf0, nf1, a1, w1_0, w2_0, w1_1, w2_1):
    a0 = sage_gcn(f64(nf0), f64(nf1), f64(w1_0), f64(w2_0))
    return sage_gcn(a0, f64(a1), f64(w1_1), f64(w2_1))

@@ -1,0 +1,274 @@
+from contextlib import ExitStack
+
+import concourse.mybir as mybir
+from concourse.masks import make_identity
+
+F32 = mybir.dt.float32
+BF16 = mybir.dt.bfloat16
+U32 = mybir.dt.uint32
+U8 = mybir.dt.uint8
+FP8X4 = mybir.dt.float8_e4m3fn_x4
+ACT = mybir.ActivationFunctionType
+ALU = mybir.AluOpType
+
+P = 128
+B, D, H1, H2 = 4096, 1024, 512, 128
+FLOPS = 2 * B * (2 * D * H1 + 2 * H1 * H2)
+NP = B // (2 * P)
+LA = 4
+
+
+def tile_graphsage_pb_t_kernel(tc, nf0, nf1, a1, w1_0, w2_0, w1_1, w2_1, out):
+    nc = tc.nc
+    with ExitStack() as ctx:
+        const = ctx.enter_context(tc.tile_pool(name="const", bufs=1))
+        wraw_pool = ctx.enter_context(tc.tile_pool(name="wraw", bufs=4))
+        wgrp_pool = ctx.enter_context(tc.tile_pool(name="wgrp", bufs=3))
+        loads = ctx.enter_context(tc.tile_pool(name="loads", bufs=LA + 1))
+        sums = ctx.enter_context(tc.tile_pool(name="sums", bufs=3))
+        grp = ctx.enter_context(tc.tile_pool(name="grp", bufs=2))
+        cod = ctx.enter_context(tc.tile_pool(name="cod", bufs=3))
+        outp = ctx.enter_context(tc.tile_pool(name="outp", bufs=2))
+        psum = ctx.enter_context(tc.psum_pool(name="psum", bufs=1))
+        ctx.enter_context(tc.manual_schedule())
+
+        nf0_v = nf0.rearrange("(p x) k -> p (x k)", p=P)
+        nf1_v = nf1.rearrange("(p x) k -> p (x k)", p=P)
+        a1_v = a1.rearrange("(p x) k -> p (x k)", p=P)
+        out_v = out.rearrange("(p x) c -> p (x c)", p=P)
+
+        ident_f = const.tile([P, P], F32, name="ident_f")
+        make_identity(nc, ident_f[:])
+        ident_b = const.tile([P, P], BF16, name="ident_b")
+        make_identity(nc, ident_b[:])
+
+        wc1 = const.tile([P, 4, H1], U32, name="wc1", align_bytes=64)
+        ws1 = const.tile([P, 4, H1], U8, name="ws1", align_bytes=64)
+        wc2 = const.tile([P, 2, H2], U32, name="wc2", align_bytes=64)
+        ws2 = const.tile([P, 2, H2], U8, name="ws2", align_bytes=64)
+
+        st = {}
+
+        def load(n):
+            t1 = loads.tile([P, 4 * D], BF16, name="nf1_t", tag="nf1")
+            nc.sync.dma_start(out=t1[:], in_=nf1_v[:, 4 * D * n : 4 * D * (n + 1)])
+            ta1 = loads.tile([P, 4 * H1], BF16, name="a1_t", tag="a1")
+            nc.sync.dma_start(out=ta1[:], in_=a1_v[:, 4 * H1 * n : 4 * H1 * (n + 1)])
+            t0 = loads.tile([P, 2 * D], BF16, name="nf0_t", tag="nf0")
+            nc.sync.dma_start(out=t0[:], in_=nf0_v[:, 2 * D * n : 2 * D * (n + 1)])
+            st[("nf1", n)] = t1
+            st[("a1", n)] = ta1
+            st[("nf0", n)] = t0
+
+        wraw = []
+
+        def load_weights():
+            for q in range(4):
+                raw = wraw_pool.tile([P, 4, H1], BF16, name="wraw", tag="wraw")
+                if q < 2:
+                    src = w2_0[512 * q : 512 * (q + 1), :].rearrange("(u w e) h -> w u e h", u=2, w=P, e=2)
+                    dst = raw[:].rearrange("w (u e) h -> w u e h", u=2, e=2)
+                else:
+                    src = w1_0[512 * (q - 2) : 512 * (q - 1), :].rearrange("(t w) h -> w t h", t=4)
+                    dst = raw[:]
+                nc.sync.dma_start(out=dst, in_=src)
+                wraw.append(raw)
+            for w in (w2_1, w1_1):
+                raw = wraw_pool.tile([P, 4, H2], BF16, name="wraw2", tag="wraw2", bufs=2)
+                nc.sync.dma_start(out=raw[:], in_=w.rearrange("(t w) c -> w t c", t=4))
+                wraw.append(raw)
+
+        wgrp = []
+
+        def w_copy(q):
+            width = H1 if q < 4 else H2
+            wg = wgrp_pool.tile([P, width, 4], BF16, name="wg", tag="wg%d" % width, align_bytes=64)
+            nc.vector.tensor_copy(
+                out=wg[:].rearrange("p (c i) t -> p c t i", i=4),
+                in_=wraw[q][:].rearrange("p t (c i) -> p c t i", i=4),
+            )
+            wgrp.append(wg)
+
+        def w_quant(q):
+            flat = wgrp[q][:].rearrange("p h t -> p (h t)")
+            if q < 4:
+                nc.vector.quantize_mx(out=wc1[:, q, :].bitcast(FP8X4), scales=ws1[:, q, :], in_=flat)
+            else:
+                nc.vector.quantize_mx(out=wc2[:, q - 4, :].bitcast(FP8X4), scales=ws2[:, q - 4, :], in_=flat)
+
+        def add_pairs(n):
+            s0 = sums.tile([P, 2, D], BF16, name="s0", tag="s0")
+            v = st[("nf1", n)][:].rearrange("p (j s k) -> p j s k", j=2, s=2)
+            nc.vector.tensor_tensor(out=s0[:], in0=v[:, :, 0, :], in1=v[:, :, 1, :], op=ALU.add)
+            s1 = sums.tile([P, 2, H1], BF16, name="s1", tag="s1")
+            v = st[("a1", n)][:].rearrange("p (j s k) -> p j s k", j=2, s=2)
+            nc.vector.tensor_tensor(out=s1[:], in0=v[:, :, 0, :], in1=v[:, :, 1, :], op=ALU.add)
+            st[("s0", n)] = s0
+            st[("s1", n)] = s1
+
+        def transposes(n):
+            s0 = st[("s0", n)]
+            s1 = st[("s1", n)]
+            x32 = st[("nf0", n)][:].bitcast(F32)
+            for j in range(2):
+                ta = psum.tile([P, 2, 4, P], BF16, name="ta%d" % j, tag="ta%d" % j)
+                for g in range(2):
+                    for t in range(4):
+                        k0 = 512 * g + 128 * t
+                        nc.tensor.transpose(ta[:, g, t, :], s0[:, j, k0 : k0 + P], ident_b[:])
+                st[("ta", n, j)] = ta
+            tb = psum.tile([P, 2, 4, P], BF16, name="tb", tag="tb")
+            for j in range(2):
+                for t in range(4):
+                    nc.tensor.transpose(tb[:, j, t, :], s1[:, j, 128 * t : 128 * (t + 1)], ident_b[:])
+            st[("tb", n)] = tb
+            for j in range(2):
+                tn = psum.tile([P, 2, 2, P], F32, name="tn%d" % j, tag="tn%d" % j)
+                for g in range(2):
+                    for u in range(2):
+                        c0 = 512 * j + 256 * g + 128 * u
+                        nc.tensor.transpose(tn[:, g, u, :], x32[:, c0 : c0 + P], ident_f[:])
+                st[("tn", n, j)] = tn
+
+        def evacuate(n):
+            gm = grp.tile([P, 2 * 4 * P * 4], BF16, name="gm", tag="gm", align_bytes=64)
+            gm5 = gm[:].rearrange("p (j q b t) -> p j q b t", j=2, q=4, b=P, t=4)
+            gm32 = gm[:].bitcast(F32).rearrange("p (j q b u) -> p j q b u", j=2, q=4, b=P, u=2)
+            for j in range(2):
+                nc.scalar.activation(
+                    out=gm5[:, j, 2:4, :, :],
+                    in_=st[("ta", n, j)][:].rearrange("p g t b -> p g b t"),
+                    func=ACT.Copy,
+                    scale=0.5,
+                )
+            g1 = grp.tile([P, 2 * P * 4], BF16, name="g1", tag="g1", align_bytes=64)
+            nc.scalar.activation(
+                out=g1[:].rearrange("p (j b t) -> p j b t", j=2, b=P, t=4),
+                in_=st[("tb", n)][:].rearrange("p j t b -> p j b t"),
+                func=ACT.Copy,
+                scale=0.5,
+            )
+            for j in range(2):
+                nc.vector.tensor_copy(
+                    out=gm32[:, j, 0:2, :, :],
+                    in_=st[("tn", n, j)][:].rearrange("p g u b -> p g b u"),
+                )
+            st[("gm", n)] = gm
+            st[("g1", n)] = g1
+
+        def quantise(n):
+            gm = st[("gm", n)]
+            cm = cod.tile([P, 8 * P], U32, name="cm", tag="cm", align_bytes=64)
+            sm = cod.tile([P, 8 * P], U8, name="sm", tag="sm", align_bytes=64)
+            for j in range(2):
+                nc.vector.quantize_mx(
+                    out=cm[:, 512 * j : 512 * (j + 1)].bitcast(FP8X4),
+                    scales=sm[:, 512 * j : 512 * (j + 1)],
+                    in_=gm[:, 2048 * j : 2048 * (j + 1)],
+                )
+            c1 = cod.tile([P, 2 * P], U32, name="c1", tag="c1", align_bytes=64)
+            sc1 = cod.tile([P, 2 * P], U8, name="sc1", tag="sc1", align_bytes=64)
+            nc.vector.quantize_mx(out=c1[:].bitcast(FP8X4), scales=sc1[:], in_=st[("g1", n)][:])
+            st[("cm", n)] = cm
+            st[("sm", n)] = sm
+            st[("c1", n)] = c1
+            st[("sc1", n)] = sc1
+
+        def layer1(n):
+            cm = st[("cm", n)]
+            sm = st[("sm", n)]
+            ga = grp.tile([P, 2 * P * 4], BF16, name="ga", tag="ga", align_bytes=64)
+            gav = ga[:].rearrange("p (j b t) -> p j b t", j=2, b=P, t=4)
+            for j in range(2):
+                acc = psum.tile([P, 4, P], F32, name="acc%d" % j, tag="acc%d" % j)
+                for t in range(4):
+                    for q in range(4):
+                        c0 = 512 * j + 128 * q
+                        nc.tensor.matmul_mx(
+                            out=acc[:, t, :],
+                            lhsT=wc1[:, q, 128 * t : 128 * (t + 1)].bitcast(FP8X4),
+                            lhsT_scale=ws1[:, q, 128 * t : 128 * (t + 1)],
+                            rhs=cm[:, c0 : c0 + P].bitcast(FP8X4),
+                            rhs_scale=sm[:, c0 : c0 + P],
+                            start=(q == 0),
+                            stop=(q == 3),
+                        )
+                nc.scalar.activation(out=gav[:, j, :, :], in_=acc[:].rearrange("p t b -> p b t"), func=ACT.Relu)
+            st[("ga", n)] = ga
+
+        def quantise_a0(n):
+            ca = cod.tile([P, 2 * P], U32, name="ca", tag="ca", align_bytes=64)
+            sa = cod.tile([P, 2 * P], U8, name="sa", tag="sa", align_bytes=64)
+            nc.vector.quantize_mx(out=ca[:].bitcast(FP8X4), scales=sa[:], in_=st[("ga", n)][:])
+            st[("ca", n)] = ca
+            st[("sa", n)] = sa
+
+        def layer2(n):
+            if n % 2 == 0:
+                ob = psum.tile([P, 4, P], F32, name="ob", tag="ob")
+                st["ob"] = ob
+            ob = st["ob"]
+            for j in range(2):
+                sub = 2 * (n % 2) + j
+                cols = slice(128 * j, 128 * (j + 1))
+                nc.tensor.matmul_mx(
+                    out=ob[:, sub, :],
+                    lhsT=st[("ca", n)][:, cols].bitcast(FP8X4),
+                    lhsT_scale=st[("sa", n)][:, cols],
+                    rhs=wc2[:, 0, :].bitcast(FP8X4),
+                    rhs_scale=ws2[:, 0, :],
+                    start=True,
+                    stop=False,
+                )
+                nc.tensor.matmul_mx(
+                    out=ob[:, sub, :],
+                    lhsT=st[("c1", n)][:, cols].bitcast(FP8X4),
+                    lhsT_scale=st[("sc1", n)][:, cols],
+                    rhs=wc2[:, 1, :].bitcast(FP8X4),
+                    rhs_scale=ws2[:, 1, :],
+                    start=False,
+                    stop=True,
+                )
+            if n % 2 == 1:
+                m = n // 2
+                ot = outp.tile([P, 4 * H2], F32, name="ot", tag="ot")
+                nc.scalar.activation(out=ot[:], in_=ob[:].rearrange("p s c -> p (s c)"), func=ACT.Relu)
+                nc.sync.dma_start(out=out_v[:, 512 * m : 512 * (m + 1)], in_=ot[:])
+
+        load(0)
+        load_weights()
+        for n in range(1, LA):
+            load(n)
+        add_pairs(0)
+        for i in range(NP + 2):
+            if i + LA < NP:
+                load(i + LA)
+            if i >= 2:
+                quantise_a0(i - 2)
+            if 1 <= i < NP - 1:
+                add_pairs(i + 1)
+            if i == 1:
+                layer1(0)
+            if i < NP:
+                transposes(i)
+                if i == 0:
+                    w_copy(0)
+                    w_copy(1)
+                    w_quant(0)
+                    w_copy(2)
+                    w_quant(1)
+                    w_copy(3)
+                    w_quant(2)
+                    w_copy(4)
+                    w_quant(3)
+                    w_copy(5)
+                    w_quant(4)
+                    w_quant(5)
+                evacuate(i)
+                quantise(i)
+            if i == 0:
+                add_pairs(1)
+            if 2 <= i <= NP:
+                layer1(i - 1)
+            if i >= 2:
+                layer2(i - 2)

@@ -14,8 +14,9 @@ ALU = mybir.AluOpType
 P = 128
 B, D, H1, H2 = 4096, 1024, 512, 128
 FLOPS = 2 * B * (2 * D * H1 + 2 * H1 * H2)
-NP = B // (2 * P)
-LA = 4
+UNIT_LENS = [1, 1, 1, 1] + [2] * 12 + [1, 1, 1, 1]
+STORE_LENS = [4] * 7 + [2, 1, 1]
+LA = 5
 
 
 def tile_graphsage_pb_t_kernel(tc, nf0, nf1, a1, w1_0, w2_0, w1_1, w2_1, out):
@@ -48,21 +49,30 @@ def tile_graphsage_pb_t_kernel(tc, nf0, nf1, a1, w1_0, w2_0, w1_1, w2_1, out):
         ws2 = const.tile([P, 2, H2], U8, name="ws2", align_bytes=64)
 
         st = {}
+        units = []
+        for length in UNIT_LENS:
+            units.append((sum(u[1] for u in units), length))
+        nu = len(units)
+        store_end = {}
+        for length in STORE_LENS:
+            first = sum(v[1] for v in store_end.values())
+            store_end[first + length - 1] = (first, length)
 
         def load(n):
-            t1 = loads.tile([P, 4 * D], BF16, name="nf1_t", tag="nf1")
-            nc.sync.dma_start(out=t1[:], in_=nf1_v[:, 4 * D * n : 4 * D * (n + 1)])
-            ta1 = loads.tile([P, 4 * H1], BF16, name="a1_t", tag="a1")
-            nc.sync.dma_start(out=ta1[:], in_=a1_v[:, 4 * H1 * n : 4 * H1 * (n + 1)])
-            t0 = loads.tile([P, 2 * D], BF16, name="nf0_t", tag="nf0")
-            nc.sync.dma_start(out=t0[:], in_=nf0_v[:, 2 * D * n : 2 * D * (n + 1)])
+            x0, ln = units[n]
+            t1 = loads.tile([P, 2 * D * ln], BF16, name="nf1_t", tag="nf1")
+            nc.sync.dma_start(out=t1[:], in_=nf1_v[:, 2 * D * x0 : 2 * D * (x0 + ln)])
+            ta1 = loads.tile([P, 2 * H1 * ln], BF16, name="a1_t", tag="a1")
+            nc.sync.dma_start(out=ta1[:], in_=a1_v[:, 2 * H1 * x0 : 2 * H1 * (x0 + ln)])
+            t0 = loads.tile([P, D * ln], BF16, name="nf0_t", tag="nf0")
+            nc.sync.dma_start(out=t0[:], in_=nf0_v[:, D * x0 : D * (x0 + ln)])
             st[("nf1", n)] = t1
             st[("a1", n)] = ta1
             st[("nf0", n)] = t0
 
         wraw = []
 
-        def load_weights():
+        def load_weights_1():
             for q in range(4):
                 raw = wraw_pool.tile([P, 4, H1], BF16, name="wraw", tag="wraw")
                 if q < 2:
@@ -73,21 +83,25 @@ def tile_graphsage_pb_t_kernel(tc, nf0, nf1, a1, w1_0, w2_0, w1_1, w2_1, out):
                     dst = raw[:]
                 nc.sync.dma_start(out=dst, in_=src)
                 wraw.append(raw)
+
+        def load_weights_2():
             for w in (w2_1, w1_1):
                 raw = wraw_pool.tile([P, 4, H2], BF16, name="wraw2", tag="wraw2", bufs=2)
                 nc.sync.dma_start(out=raw[:], in_=w.rearrange("(t w) c -> w t c", t=4))
                 wraw.append(raw)
 
-        wgrp = []
+        wgrp = {}
 
-        def w_copy(q):
+        def w_copy(q, on_scalar):
             width = H1 if q < 4 else H2
             wg = wgrp_pool.tile([P, width, 4], BF16, name="wg", tag="wg%d" % width, align_bytes=64)
-            nc.vector.tensor_copy(
-                out=wg[:].rearrange("p (c i) t -> p c t i", i=4),
-                in_=wraw[q][:].rearrange("p t (c i) -> p c t i", i=4),
-            )
-            wgrp.append(wg)
+            dst = wg[:].rearrange("p (c i) t -> p c t i", i=4)
+            src = wraw[q][:].rearrange("p t (c i) -> p c t i", i=4)
+            if on_scalar:
+                nc.scalar.copy(out=dst, in_=src)
+            else:
+                nc.vector.tensor_copy(out=dst, in_=src)
+            wgrp[q] = wg
 
         def w_quant(q):
             flat = wgrp[q][:].rearrange("p h t -> p (h t)")
@@ -97,20 +111,22 @@ def tile_graphsage_pb_t_kernel(tc, nf0, nf1, a1, w1_0, w2_0, w1_1, w2_1, out):
                 nc.vector.quantize_mx(out=wc2[:, q - 4, :].bitcast(FP8X4), scales=ws2[:, q - 4, :], in_=flat)
 
         def add_pairs(n):
-            s0 = sums.tile([P, 2, D], BF16, name="s0", tag="s0")
-            v = st[("nf1", n)][:].rearrange("p (j s k) -> p j s k", j=2, s=2)
+            ln = units[n][1]
+            s0 = sums.tile([P, ln, D], BF16, name="s0", tag="s0")
+            v = st[("nf1", n)][:].rearrange("p (j s k) -> p j s k", j=ln, s=2)
             nc.vector.tensor_tensor(out=s0[:], in0=v[:, :, 0, :], in1=v[:, :, 1, :], op=ALU.add)
-            s1 = sums.tile([P, 2, H1], BF16, name="s1", tag="s1")
-            v = st[("a1", n)][:].rearrange("p (j s k) -> p j s k", j=2, s=2)
+            s1 = sums.tile([P, ln, H1], BF16, name="s1", tag="s1")
+            v = st[("a1", n)][:].rearrange("p (j s k) -> p j s k", j=ln, s=2)
             nc.vector.tensor_tensor(out=s1[:], in0=v[:, :, 0, :], in1=v[:, :, 1, :], op=ALU.add)
             st[("s0", n)] = s0
             st[("s1", n)] = s1
 
         def transposes(n):
+            ln = units[n][1]
             s0 = st[("s0", n)]
             s1 = st[("s1", n)]
             x32 = st[("nf0", n)][:].bitcast(F32)
-            for j in range(2):
+            for j in range(ln):
                 ta = psum.tile([P, 2, 4, P], BF16, name="ta%d" % j, tag="ta%d" % j)
                 for g in range(2):
                     for t in range(4):
@@ -118,11 +134,11 @@ def tile_graphsage_pb_t_kernel(tc, nf0, nf1, a1, w1_0, w2_0, w1_1, w2_1, out):
                         nc.tensor.transpose(ta[:, g, t, :], s0[:, j, k0 : k0 + P], ident_b[:])
                 st[("ta", n, j)] = ta
             tb = psum.tile([P, 2, 4, P], BF16, name="tb", tag="tb")
-            for j in range(2):
+            for j in range(ln):
                 for t in range(4):
                     nc.tensor.transpose(tb[:, j, t, :], s1[:, j, 128 * t : 128 * (t + 1)], ident_b[:])
             st[("tb", n)] = tb
-            for j in range(2):
+            for j in range(ln):
                 tn = psum.tile([P, 2, 2, P], F32, name="tn%d" % j, tag="tn%d" % j)
                 for g in range(2):
                     for u in range(2):
@@ -131,24 +147,25 @@ def tile_graphsage_pb_t_kernel(tc, nf0, nf1, a1, w1_0, w2_0, w1_1, w2_1, out):
                 st[("tn", n, j)] = tn
 
         def evacuate(n):
-            gm = grp.tile([P, 2 * 4 * P * 4], BF16, name="gm", tag="gm", align_bytes=64)
-            gm5 = gm[:].rearrange("p (j q b t) -> p j q b t", j=2, q=4, b=P, t=4)
-            gm32 = gm[:].bitcast(F32).rearrange("p (j q b u) -> p j q b u", j=2, q=4, b=P, u=2)
-            for j in range(2):
+            ln = units[n][1]
+            gm = grp.tile([P, ln * 4 * P * 4], BF16, name="gm", tag="gm", align_bytes=64)
+            gm5 = gm[:].rearrange("p (j q b t) -> p j q b t", j=ln, q=4, b=P, t=4)
+            gm32 = gm[:].bitcast(F32).rearrange("p (j q b u) -> p j q b u", j=ln, q=4, b=P, u=2)
+            for j in range(ln):
                 nc.scalar.activation(
                     out=gm5[:, j, 2:4, :, :],
                     in_=st[("ta", n, j)][:].rearrange("p g t b -> p g b t"),
                     func=ACT.Copy,
                     scale=0.5,
                 )
-            g1 = grp.tile([P, 2 * P * 4], BF16, name="g1", tag="g1", align_bytes=64)
+            g1 = grp.tile([P, ln * P * 4], BF16, name="g1", tag="g1", align_bytes=64)
             nc.scalar.activation(
-                out=g1[:].rearrange("p (j b t) -> p j b t", j=2, b=P, t=4),
-                in_=st[("tb", n)][:].rearrange("p j t b -> p j b t"),
+                out=g1[:].rearrange("p (j b t) -> p j b t", j=ln, b=P, t=4),
+                in_=st[("tb", n)][:, 0:ln, :, :].rearrange("p j t b -> p j b t"),
                 func=ACT.Copy,
                 scale=0.5,
             )
-            for j in range(2):
+            for j in range(ln):
                 nc.vector.tensor_copy(
                     out=gm32[:, j, 0:2, :, :],
                     in_=st[("tn", n, j)][:].rearrange("p g u b -> p g b u"),
@@ -157,17 +174,18 @@ def tile_graphsage_pb_t_kernel(tc, nf0, nf1, a1, w1_0, w2_0, w1_1, w2_1, out):
             st[("g1", n)] = g1
 
         def quantise(n):
+            ln = units[n][1]
             gm = st[("gm", n)]
-            cm = cod.tile([P, 8 * P], U32, name="cm", tag="cm", align_bytes=64)
-            sm = cod.tile([P, 8 * P], U8, name="sm", tag="sm", align_bytes=64)
-            for j in range(2):
+            cm = cod.tile([P, ln * 4 * P], U32, name="cm", tag="cm", align_bytes=64)
+            sm = cod.tile([P, ln * 4 * P], U8, name="sm", tag="sm", align_bytes=64)
+            for j in range(ln):
                 nc.vector.quantize_mx(
                     out=cm[:, 512 * j : 512 * (j + 1)].bitcast(FP8X4),
                     scales=sm[:, 512 * j : 512 * (j + 1)],
                     in_=gm[:, 2048 * j : 2048 * (j + 1)],
                 )
-            c1 = cod.tile([P, 2 * P], U32, name="c1", tag="c1", align_bytes=64)
-            sc1 = cod.tile([P, 2 * P], U8, name="sc1", tag="sc1", align_bytes=64)
+            c1 = cod.tile([P, ln * P], U32, name="c1", tag="c1", align_bytes=64)
+            sc1 = cod.tile([P, ln * P], U8, name="sc1", tag="sc1", align_bytes=64)
             nc.vector.quantize_mx(out=c1[:].bitcast(FP8X4), scales=sc1[:], in_=st[("g1", n)][:])
             st[("cm", n)] = cm
             st[("sm", n)] = sm
@@ -175,11 +193,12 @@ def tile_graphsage_pb_t_kernel(tc, nf0, nf1, a1, w1_0, w2_0, w1_1, w2_1, out):
             st[("sc1", n)] = sc1
 
         def layer1(n):
+            ln = units[n][1]
             cm = st[("cm", n)]
             sm = st[("sm", n)]
-            ga = grp.tile([P, 2 * P * 4], BF16, name="ga", tag="ga", align_bytes=64)
-            gav = ga[:].rearrange("p (j b t) -> p j b t", j=2, b=P, t=4)
-            for j in range(2):
+            ga = grp.tile([P, ln * P * 4], BF16, name="ga", tag="ga", align_bytes=64)
+            gav = ga[:].rearrange("p (j b t) -> p j b t", j=ln, b=P, t=4)
+            for j in range(ln):
                 acc = psum.tile([P, 4, P], F32, name="acc%d" % j, tag="acc%d" % j)
                 for t in range(4):
                     for q in range(4):
@@ -197,22 +216,24 @@ def tile_graphsage_pb_t_kernel(tc, nf0, nf1, a1, w1_0, w2_0, w1_1, w2_1, out):
             st[("ga", n)] = ga
 
         def quantise_a0(n):
-            ca = cod.tile([P, 2 * P], U32, name="ca", tag="ca", align_bytes=64)
-            sa = cod.tile([P, 2 * P], U8, name="sa", tag="sa", align_bytes=64)
+            ln = units[n][1]
+            ca = cod.tile([P, ln * P], U32, name="ca", tag="ca", align_bytes=64)
+            sa = cod.tile([P, ln * P], U8, name="sa", tag="sa", align_bytes=64)
             nc.vector.quantize_mx(out=ca[:].bitcast(FP8X4), scales=sa[:], in_=st[("ga", n)][:])
             st[("ca", n)] = ca
             st[("sa", n)] = sa
 
         def layer2(n):
-            if n % 2 == 0:
-                ob = psum.tile([P, 4, P], F32, name="ob", tag="ob")
-                st["ob"] = ob
-            ob = st["ob"]
-            for j in range(2):
-                sub = 2 * (n % 2) + j
+            x0, ln = units[n]
+            for j in range(ln):
+                x = x0 + j
+                if x % 4 == 0:
+                    ob_new = psum.tile([P, 4, P], F32, name="ob", tag="ob")
+                    st["ob"] = ob_new
+                ob = st["ob"]
                 cols = slice(128 * j, 128 * (j + 1))
                 nc.tensor.matmul_mx(
-                    out=ob[:, sub, :],
+                    out=ob[:, x % 4, :],
                     lhsT=st[("ca", n)][:, cols].bitcast(FP8X4),
                     lhsT_scale=st[("sa", n)][:, cols],
                     rhs=wc2[:, 0, :].bitcast(FP8X4),
@@ -221,7 +242,7 @@ def tile_graphsage_pb_t_kernel(tc, nf0, nf1, a1, w1_0, w2_0, w1_1, w2_1, out):
                     stop=False,
                 )
                 nc.tensor.matmul_mx(
-                    out=ob[:, sub, :],
+                    out=ob[:, x % 4, :],
                     lhsT=st[("c1", n)][:, cols].bitcast(FP8X4),
                     lhsT_scale=st[("sc1", n)][:, cols],
                     rhs=wc2[:, 1, :].bitcast(FP8X4),
@@ -229,46 +250,46 @@ def tile_graphsage_pb_t_kernel(tc, nf0, nf1, a1, w1_0, w2_0, w1_1, w2_1, out):
                     start=False,
                     stop=True,
                 )
-            if n % 2 == 1:
-                m = n // 2
-                ot = outp.tile([P, 4 * H2], F32, name="ot", tag="ot")
-                nc.scalar.activation(out=ot[:], in_=ob[:].rearrange("p s c -> p (s c)"), func=ACT.Relu)
-                nc.sync.dma_start(out=out_v[:, 512 * m : 512 * (m + 1)], in_=ot[:])
+                if x in store_end:
+                    first, length = store_end[x]
+                    ot = outp.tile([P, length, H2], F32, name="ot", tag="ot")
+                    nc.scalar.activation(out=ot[:], in_=ob[:, first % 4 : first % 4 + length, :], func=ACT.Relu)
+                    nc.sync.dma_start(
+                        out=out_v[:, H2 * first : H2 * (first + length)], in_=ot[:].rearrange("p s c -> p (s c)")
+                    )
 
+        load_weights_1()
         load(0)
-        load_weights()
-        for n in range(1, LA):
+        load(1)
+        load_weights_2()
+        for n in range(2, LA):
             load(n)
+        w_copy(0, False)
+        w_copy(1, True)
+        w_quant(0)
+        w_copy(2, False)
+        w_copy(3, True)
+        w_quant(1)
+        w_quant(2)
         add_pairs(0)
-        for i in range(NP + 2):
-            if i + LA < NP:
+        w_quant(3)
+        for i in range(nu + 2):
+            if i + LA < nu:
                 load(i + LA)
             if i >= 2:
                 quantise_a0(i - 2)
-            if 1 <= i < NP - 1:
+            if i + 1 < nu:
                 add_pairs(i + 1)
-            if i == 1:
-                layer1(0)
-            if i < NP:
+            if i < nu:
                 transposes(i)
-                if i == 0:
-                    w_copy(0)
-                    w_copy(1)
-                    w_quant(0)
-                    w_copy(2)
-                    w_quant(1)
-                    w_copy(3)
-                    w_quant(2)
-                    w_copy(4)
-                    w_quant(3)
-                    w_copy(5)
-                    w_quant(4)
-                    w_quant(5)
                 evacuate(i)
                 quantise(i)
             if i == 0:
-                add_pairs(1)
-            if 2 <= i <= NP:
+                w_copy(4, False)
+                w_copy(5, False)
+                w_quant(4)
+                w_quant(5)
+            if 1 <= i <= nu:
                 layer1(i - 1)
             if i >= 2:
                 layer2(i - 2)

@@ -16,6 +16,7 @@ B, D, H1, H2 = 4096, 1024, 512, 128
 FLOPS = 2 * B * (2 * D * H1 + 2 * H1 * H2)
 UNIT_LENS = [1, 1, 1, 1] + [2] * 12 + [1, 1, 1, 1]
 STORE_LENS = [4] * 7 + [2, 1, 1]
+SPLIT = True
 LA = 5
 
 
@@ -121,11 +122,9 @@ def tile_graphsage_pb_t_kernel(tc, nf0, nf1, a1, w1_0, w2_0, w1_1, w2_1, out):
             st[("s0", n)] = s0
             st[("s1", n)] = s1
 
-        def transposes(n):
+        def transposes_a(n):
             ln = units[n][1]
             s0 = st[("s0", n)]
-            s1 = st[("s1", n)]
-            x32 = st[("nf0", n)][:].bitcast(F32)
             for j in range(ln):
                 ta = psum.tile([P, 2, 4, P], BF16, name="ta%d" % j, tag="ta%d" % j)
                 for g in range(2):
@@ -133,6 +132,11 @@ def tile_graphsage_pb_t_kernel(tc, nf0, nf1, a1, w1_0, w2_0, w1_1, w2_1, out):
                         k0 = 512 * g + 128 * t
                         nc.tensor.transpose(ta[:, g, t, :], s0[:, j, k0 : k0 + P], ident_b[:])
                 st[("ta", n, j)] = ta
+
+        def transposes_b(n):
+            ln = units[n][1]
+            s1 = st[("s1", n)]
+            x32 = st[("nf0", n)][:].bitcast(F32)
             tb = psum.tile([P, 2, 4, P], BF16, name="tb", tag="tb")
             for j in range(ln):
                 for t in range(4):
@@ -146,11 +150,11 @@ def tile_graphsage_pb_t_kernel(tc, nf0, nf1, a1, w1_0, w2_0, w1_1, w2_1, out):
                         nc.tensor.transpose(tn[:, g, u, :], x32[:, c0 : c0 + P], ident_f[:])
                 st[("tn", n, j)] = tn
 
-        def evacuate(n):
+        def evacuate_a(n):
             ln = units[n][1]
             gm = grp.tile([P, ln * 4 * P * 4], BF16, name="gm", tag="gm", align_bytes=64)
+            st[("gm", n)] = gm
             gm5 = gm[:].rearrange("p (j q b t) -> p j q b t", j=ln, q=4, b=P, t=4)
-            gm32 = gm[:].bitcast(F32).rearrange("p (j q b u) -> p j q b u", j=ln, q=4, b=P, u=2)
             for j in range(ln):
                 nc.scalar.activation(
                     out=gm5[:, j, 2:4, :, :],
@@ -158,6 +162,11 @@ def tile_graphsage_pb_t_kernel(tc, nf0, nf1, a1, w1_0, w2_0, w1_1, w2_1, out):
                     func=ACT.Copy,
                     scale=0.5,
                 )
+
+        def evacuate_b(n):
+            ln = units[n][1]
+            gm = st[("gm", n)]
+            gm32 = gm[:].bitcast(F32).rearrange("p (j q b u) -> p j q b u", j=ln, q=4, b=P, u=2)
             g1 = grp.tile([P, ln * P * 4], BF16, name="g1", tag="g1", align_bytes=64)
             nc.scalar.activation(
                 out=g1[:].rearrange("p (j b t) -> p j b t", j=ln, b=P, t=4),
@@ -170,7 +179,6 @@ def tile_graphsage_pb_t_kernel(tc, nf0, nf1, a1, w1_0, w2_0, w1_1, w2_1, out):
                     out=gm32[:, j, 0:2, :, :],
                     in_=st[("tn", n, j)][:].rearrange("p g u b -> p g b u"),
                 )
-            st[("gm", n)] = gm
             st[("g1", n)] = g1
 
         def quantise(n):
@@ -192,13 +200,16 @@ def tile_graphsage_pb_t_kernel(tc, nf0, nf1, a1, w1_0, w2_0, w1_1, w2_1, out):
             st[("c1", n)] = c1
             st[("sc1", n)] = sc1
 
-        def layer1(n):
+        def layer1(n, js):
             ln = units[n][1]
             cm = st[("cm", n)]
             sm = st[("sm", n)]
-            ga = grp.tile([P, ln * P * 4], BF16, name="ga", tag="ga", align_bytes=64)
+            if 0 in js:
+                ga_new = grp.tile([P, ln * P * 4], BF16, name="ga", tag="ga", align_bytes=64)
+                st[("ga", n)] = ga_new
+            ga = st[("ga", n)]
             gav = ga[:].rearrange("p (j b t) -> p j b t", j=ln, b=P, t=4)
-            for j in range(ln):
+            for j in js:
                 acc = psum.tile([P, 4, P], F32, name="acc%d" % j, tag="acc%d" % j)
                 for t in range(4):
                     for q in range(4):
@@ -213,7 +224,6 @@ def tile_graphsage_pb_t_kernel(tc, nf0, nf1, a1, w1_0, w2_0, w1_1, w2_1, out):
                             stop=(q == 3),
                         )
                 nc.scalar.activation(out=gav[:, j, :, :], in_=acc[:].rearrange("p t b -> p b t"), func=ACT.Relu)
-            st[("ga", n)] = ga
 
         def quantise_a0(n):
             ln = units[n][1]
@@ -280,9 +290,14 @@ def tile_graphsage_pb_t_kernel(tc, nf0, nf1, a1, w1_0, w2_0, w1_1, w2_1, out):
                 quantise_a0(i - 2)
             if i + 1 < nu:
                 add_pairs(i + 1)
+            split = SPLIT and 1 <= i < nu and units[i][1] == 2 and units[i - 1][1] == 2
             if i < nu:
-                transposes(i)
-                evacuate(i)
+                transposes_a(i)
+                evacuate_a(i)
+                if split:
+                    layer1(i - 1, [0])
+                transposes_b(i)
+                evacuate_b(i)
                 quantise(i)
             if i == 0:
                 w_copy(4, False)
@@ -290,6 +305,6 @@ def tile_graphsage_pb_t_kernel(tc, nf0, nf1, a1, w1_0, w2_0, w1_1, w2_1, out):
                 w_quant(4)
                 w_quant(5)
             if 1 <= i <= nu:
-                layer1(i - 1)
+                layer1(i - 1, [1] if split else list(range(units[i - 1][1])))
             if i >= 2:
                 layer2(i - 2)

@@ -14,9 +14,8 @@ ALU = mybir.AluOpType
 P = 128
 B, D, H1, H2 = 4096, 1024, 512, 128
 FLOPS = 2 * B * (2 * D * H1 + 2 * H1 * H2)
-UNIT_LENS = [1, 1, 1, 1] + [2] * 12 + [1, 1, 1, 1]
-STORE_LENS = [4] * 7 + [2, 1, 1]
-SPLIT = True
+UNIT_LENS = [2] * 16
+STORE_LENS = [4] * 7 + [2, 2]
 LA = 5
 
 
@@ -122,9 +121,11 @@ def tile_graphsage_pb_t_kernel(tc, nf0, nf1, a1, w1_0, w2_0, w1_1, w2_1, out):
             st[("s0", n)] = s0
             st[("s1", n)] = s1
 
-        def transposes_a(n):
+        def transposes(n):
             ln = units[n][1]
             s0 = st[("s0", n)]
+            s1 = st[("s1", n)]
+            x32 = st[("nf0", n)][:].bitcast(F32)
             for j in range(ln):
                 ta = psum.tile([P, 2, 4, P], BF16, name="ta%d" % j, tag="ta%d" % j)
                 for g in range(2):
@@ -132,11 +133,6 @@ def tile_graphsage_pb_t_kernel(tc, nf0, nf1, a1, w1_0, w2_0, w1_1, w2_1, out):
                         k0 = 512 * g + 128 * t
                         nc.tensor.transpose(ta[:, g, t, :], s0[:, j, k0 : k0 + P], ident_b[:])
                 st[("ta", n, j)] = ta
-
-        def transposes_b(n):
-            ln = units[n][1]
-            s1 = st[("s1", n)]
-            x32 = st[("nf0", n)][:].bitcast(F32)
             tb = psum.tile([P, 2, 4, P], BF16, name="tb", tag="tb")
             for j in range(ln):
                 for t in range(4):
@@ -150,11 +146,11 @@ def tile_graphsage_pb_t_kernel(tc, nf0, nf1, a1, w1_0, w2_0, w1_1, w2_1, out):
                         nc.tensor.transpose(tn[:, g, u, :], x32[:, c0 : c0 + P], ident_f[:])
                 st[("tn", n, j)] = tn
 
-        def evacuate_a(n):
+        def evacuate(n):
             ln = units[n][1]
             gm = grp.tile([P, ln * 4 * P * 4], BF16, name="gm", tag="gm", align_bytes=64)
-            st[("gm", n)] = gm
-            gm5 = gm[:].rearrange("p (j q b t) -> p j q b t", j=ln, q=4, b=P, t=4)
+            gm5 = gm[:].rearrange("p (q j b t) -> p j q b t", j=ln, q=4, b=P, t=4)
+            gm32 = gm[:].bitcast(F32).rearrange("p (q j b u) -> p j q b u", j=ln, q=4, b=P, u=2)
             for j in range(ln):
                 nc.scalar.activation(
                     out=gm5[:, j, 2:4, :, :],
@@ -162,11 +158,6 @@ def tile_graphsage_pb_t_kernel(tc, nf0, nf1, a1, w1_0, w2_0, w1_1, w2_1, out):
                     func=ACT.Copy,
                     scale=0.5,
                 )
-
-        def evacuate_b(n):
-            ln = units[n][1]
-            gm = st[("gm", n)]
-            gm32 = gm[:].bitcast(F32).rearrange("p (j q b u) -> p j q b u", j=ln, q=4, b=P, u=2)
             g1 = grp.tile([P, ln * P * 4], BF16, name="g1", tag="g1", align_bytes=64)
             nc.scalar.activation(
                 out=g1[:].rearrange("p (j b t) -> p j b t", j=ln, b=P, t=4),
@@ -179,6 +170,7 @@ def tile_graphsage_pb_t_kernel(tc, nf0, nf1, a1, w1_0, w2_0, w1_1, w2_1, out):
                     out=gm32[:, j, 0:2, :, :],
                     in_=st[("tn", n, j)][:].rearrange("p g u b -> p g b u"),
                 )
+            st[("gm", n)] = gm
             st[("g1", n)] = g1
 
         def quantise(n):
@@ -186,11 +178,11 @@ def tile_graphsage_pb_t_kernel(tc, nf0, nf1, a1, w1_0, w2_0, w1_1, w2_1, out):
             gm = st[("gm", n)]
             cm = cod.tile([P, ln * 4 * P], U32, name="cm", tag="cm", align_bytes=64)
             sm = cod.tile([P, ln * 4 * P], U8, name="sm", tag="sm", align_bytes=64)
-            for j in range(ln):
+            for h in range(2):
                 nc.vector.quantize_mx(
-                    out=cm[:, 512 * j : 512 * (j + 1)].bitcast(FP8X4),
-                    scales=sm[:, 512 * j : 512 * (j + 1)],
-                    in_=gm[:, 2048 * j : 2048 * (j + 1)],
+                    out=cm[:, 512 * h : 512 * (h + 1)].bitcast(FP8X4),
+                    scales=sm[:, 512 * h : 512 * (h + 1)],
+                    in_=gm[:, 2048 * h : 2048 * (h + 1)],
                 )
             c1 = cod.tile([P, ln * P], U32, name="c1", tag="c1", align_bytes=64)
             sc1 = cod.tile([P, ln * P], U8, name="sc1", tag="sc1", align_bytes=64)
@@ -200,30 +192,28 @@ def tile_graphsage_pb_t_kernel(tc, nf0, nf1, a1, w1_0, w2_0, w1_1, w2_1, out):
             st[("c1", n)] = c1
             st[("sc1", n)] = sc1
 
-        def layer1(n, js):
+        def layer1(n):
             ln = units[n][1]
             cm = st[("cm", n)]
             sm = st[("sm", n)]
-            if 0 in js:
-                ga_new = grp.tile([P, ln * P * 4], BF16, name="ga", tag="ga", align_bytes=64)
-                st[("ga", n)] = ga_new
-            ga = st[("ga", n)]
-            gav = ga[:].rearrange("p (j b t) -> p j b t", j=ln, b=P, t=4)
-            for j in js:
-                acc = psum.tile([P, 4, P], F32, name="acc%d" % j, tag="acc%d" % j)
-                for t in range(4):
+            ga = grp.tile([P, ln * P * 4], BF16, name="ga", tag="ga", align_bytes=64)
+            gav = ga[:].rearrange("p (c h t) -> p h c t", c=2 * P, h=2, t=2)
+            for h in range(2):
+                acc = psum.tile([P, 2, 2 * P], F32, name="acc%d" % h, tag="acc%d" % h)
+                for t in range(2):
+                    m0 = 128 * (2 * h + t)
                     for q in range(4):
-                        c0 = 512 * j + 128 * q
                         nc.tensor.matmul_mx(
                             out=acc[:, t, :],
-                            lhsT=wc1[:, q, 128 * t : 128 * (t + 1)].bitcast(FP8X4),
-                            lhsT_scale=ws1[:, q, 128 * t : 128 * (t + 1)],
-                            rhs=cm[:, c0 : c0 + P].bitcast(FP8X4),
-                            rhs_scale=sm[:, c0 : c0 + P],
+                            lhsT=wc1[:, q, m0 : m0 + P].bitcast(FP8X4),
+                            lhsT_scale=ws1[:, q, m0 : m0 + P],
+                            rhs=cm[:, 256 * q : 256 * (q + 1)].bitcast(FP8X4),
+                            rhs_scale=sm[:, 256 * q : 256 * (q + 1)],
                             start=(q == 0),
                             stop=(q == 3),
                         )
-                nc.scalar.activation(out=gav[:, j, :, :], in_=acc[:].rearrange("p t b -> p b t"), func=ACT.Relu)
+                nc.scalar.activation(out=gav[:, h, :, :], in_=acc[:].rearrange("p t c -> p c t"), func=ACT.Relu)
+            st[("ga", n)] = ga
 
         def quantise_a0(n):
             ln = units[n][1]
@@ -263,7 +253,7 @@ def tile_graphsage_pb_t_kernel(tc, nf0, nf1, a1, w1_0, w2_0, w1_1, w2_1, out):
                 if x in store_end:
                     first, length = store_end[x]
                     ot = outp.tile([P, length, H2], F32, name="ot", tag="ot")
-                    nc.scalar.activation(out=ot[:], in_=ob[:, first % 4 : first % 4 + length, :], func=ACT.Relu)
+                    nc.vector.tensor_relu(out=ot[:], in_=ob[:, first % 4 : first % 4 + length, :])
                     nc.sync.dma_start(
                         out=out_v[:, H2 * first : H2 * (first + length)], in_=ot[:].rearrange("p s c -> p (s c)")
                     )
@@ -290,14 +280,9 @@ def tile_graphsage_pb_t_kernel(tc, nf0, nf1, a1, w1_0, w2_0, w1_1, w2_1, out):
                 quantise_a0(i - 2)
             if i + 1 < nu:
                 add_pairs(i + 1)
-            split = SPLIT and 1 <= i < nu and units[i][1] == 2 and units[i - 1][1] == 2
             if i < nu:
-                transposes_a(i)
-                evacuate_a(i)
-                if split:
-                    layer1(i - 1, [0])
-                transposes_b(i)
-                evacuate_b(i)
+                transposes(i)
+                evacuate(i)
                 quantise(i)
             if i == 0:
                 w_copy(4, False)
@@ -305,6 +290,6 @@ def tile_graphsage_pb_t_kernel(tc, nf0, nf1, a1, w1_0, w2_0, w1_1, w2_1, out):
                 w_quant(4)
                 w_quant(5)
             if 1 <= i <= nu:
-                layer1(i - 1, [1] if split else list(range(units[i - 1][1])))
+                layer1(i - 1)
             if i >= 2:
                 layer2(i - 2)

@@ -12,284 +12,260 @@ ACT = mybir.ActivationFunctionType
 ALU = mybir.AluOpType
 
 P = 128
+PACK = 4
+K_PASS = P * PACK
 B, D, H1, H2 = 4096, 1024, 512, 128
 FLOPS = 2 * B * (2 * D * H1 + 2 * H1 * H2)
-UNIT_LENS = [2] * 16
-STORE_LENS = [4] * 7 + [2, 2]
-LA = 5
+
+PAIRS = B // (2 * P)
+PAIR = 2 * P
+L1_PASSES = 2 * D // K_PASS
+AHEAD = 5
+SLICES_PER_BANK = 4
 
 
 def tile_graphsage_pb_t_kernel(tc, nf0, nf1, a1, w1_0, w2_0, w1_1, w2_1, out):
     nc = tc.nc
     with ExitStack() as ctx:
         const = ctx.enter_context(tc.tile_pool(name="const", bufs=1))
-        wraw_pool = ctx.enter_context(tc.tile_pool(name="wraw", bufs=4))
-        wgrp_pool = ctx.enter_context(tc.tile_pool(name="wgrp", bufs=3))
-        loads = ctx.enter_context(tc.tile_pool(name="loads", bufs=LA + 1))
+        weights_in = ctx.enter_context(tc.tile_pool(name="weights_in", bufs=L1_PASSES))
+        weights_grouped = ctx.enter_context(tc.tile_pool(name="weights_grouped", bufs=L1_PASSES))
+        loads = ctx.enter_context(tc.tile_pool(name="loads", bufs=AHEAD + 1))
         sums = ctx.enter_context(tc.tile_pool(name="sums", bufs=3))
-        grp = ctx.enter_context(tc.tile_pool(name="grp", bufs=2))
-        cod = ctx.enter_context(tc.tile_pool(name="cod", bufs=3))
-        outp = ctx.enter_context(tc.tile_pool(name="outp", bufs=2))
+        grouped = ctx.enter_context(tc.tile_pool(name="grouped", bufs=2))
+        codes = ctx.enter_context(tc.tile_pool(name="codes", bufs=3))
+        results = ctx.enter_context(tc.tile_pool(name="results", bufs=2))
         psum = ctx.enter_context(tc.psum_pool(name="psum", bufs=1))
         ctx.enter_context(tc.manual_schedule())
 
-        nf0_v = nf0.rearrange("(p x) k -> p (x k)", p=P)
-        nf1_v = nf1.rearrange("(p x) k -> p (x k)", p=P)
-        a1_v = a1.rearrange("(p x) k -> p (x k)", p=P)
-        out_v = out.rearrange("(p x) c -> p (x c)", p=P)
+        nf0_rows = nf0.rearrange("(p x) k -> p (x k)", p=P)
+        nf1_rows = nf1.rearrange("(p x) k -> p (x k)", p=P)
+        a1_rows = a1.rearrange("(p x) k -> p (x k)", p=P)
+        out_rows = out.rearrange("(p x) c -> p (x c)", p=P)
 
-        ident_f = const.tile([P, P], F32, name="ident_f")
-        make_identity(nc, ident_f[:])
-        ident_b = const.tile([P, P], BF16, name="ident_b")
-        make_identity(nc, ident_b[:])
+        identity_f32 = const.tile([P, P], F32, name="identity_f32")
+        make_identity(nc, identity_f32[:])
+        identity_bf16 = const.tile([P, P], BF16, name="identity_bf16")
+        make_identity(nc, identity_bf16[:])
 
-        wc1 = const.tile([P, 4, H1], U32, name="wc1", align_bytes=64)
-        ws1 = const.tile([P, 4, H1], U8, name="ws1", align_bytes=64)
-        wc2 = const.tile([P, 2, H2], U32, name="wc2", align_bytes=64)
-        ws2 = const.tile([P, 2, H2], U8, name="ws2", align_bytes=64)
+        w_l1_codes = const.tile([P, L1_PASSES, H1], U32, name="w_l1_codes", align_bytes=64)
+        w_l1_scales = const.tile([P, L1_PASSES, H1], U8, name="w_l1_scales", align_bytes=64)
+        w_l2_codes = const.tile([P, 2, H2], U32, name="w_l2_codes", align_bytes=64)
+        w_l2_scales = const.tile([P, 2, H2], U8, name="w_l2_scales", align_bytes=64)
 
-        st = {}
-        units = []
-        for length in UNIT_LENS:
-            units.append((sum(u[1] for u in units), length))
-        nu = len(units)
-        store_end = {}
-        for length in STORE_LENS:
-            first = sum(v[1] for v in store_end.values())
-            store_end[first + length - 1] = (first, length)
+        held = {}
 
-        def load(n):
-            x0, ln = units[n]
-            t1 = loads.tile([P, 2 * D * ln], BF16, name="nf1_t", tag="nf1")
-            nc.sync.dma_start(out=t1[:], in_=nf1_v[:, 2 * D * x0 : 2 * D * (x0 + ln)])
-            ta1 = loads.tile([P, 2 * H1 * ln], BF16, name="a1_t", tag="a1")
-            nc.sync.dma_start(out=ta1[:], in_=a1_v[:, 2 * H1 * x0 : 2 * H1 * (x0 + ln)])
-            t0 = loads.tile([P, D * ln], BF16, name="nf0_t", tag="nf0")
-            nc.sync.dma_start(out=t0[:], in_=nf0_v[:, D * x0 : D * (x0 + ln)])
-            st[("nf1", n)] = t1
-            st[("a1", n)] = ta1
-            st[("nf0", n)] = t0
 
-        wraw = []
-
-        def load_weights_1():
-            for q in range(4):
-                raw = wraw_pool.tile([P, 4, H1], BF16, name="wraw", tag="wraw")
-                if q < 2:
-                    src = w2_0[512 * q : 512 * (q + 1), :].rearrange("(u w e) h -> w u e h", u=2, w=P, e=2)
-                    dst = raw[:].rearrange("w (u e) h -> w u e h", u=2, e=2)
+        def load_layer1_weights():
+            for c in range(L1_PASSES):
+                raw = weights_in.tile([P, PACK, H1], BF16, name="w_l1_raw", tag="w_l1_raw")
+                if c < 2:
+                    rows = w2_0[K_PASS * c : K_PASS * (c + 1), :]
+                    nc.sync.dma_start(
+                        out=raw[:].rearrange("p (u e) h -> p u e h", u=2, e=2),
+                        in_=rows.rearrange("(u p e) h -> p u e h", u=2, p=P, e=2),
+                    )
                 else:
-                    src = w1_0[512 * (q - 2) : 512 * (q - 1), :].rearrange("(t w) h -> w t h", t=4)
-                    dst = raw[:]
-                nc.sync.dma_start(out=dst, in_=src)
-                wraw.append(raw)
+                    rows = w1_0[K_PASS * (c - 2) : K_PASS * (c - 1), :]
+                    nc.sync.dma_start(out=raw[:], in_=rows.rearrange("(t p) h -> p t h", t=PACK))
+                held[("w_raw", c)] = raw
 
-        def load_weights_2():
-            for w in (w2_1, w1_1):
-                raw = wraw_pool.tile([P, 4, H2], BF16, name="wraw2", tag="wraw2", bufs=2)
-                nc.sync.dma_start(out=raw[:], in_=w.rearrange("(t w) c -> w t c", t=4))
-                wraw.append(raw)
+        def load_layer2_weights():
+            for c, w in enumerate((w2_1, w1_1)):
+                raw = weights_in.tile([P, PACK, H2], BF16, name="w_l2_raw", tag="w_l2_raw", bufs=2)
+                nc.sync.dma_start(out=raw[:], in_=w.rearrange("(t p) c -> p t c", t=PACK))
+                held[("w_raw", L1_PASSES + c)] = raw
 
-        wgrp = {}
+        def group_weights(c, engine_copy):
+            width = H1 if c < L1_PASSES else H2
+            side_by_side = weights_grouped.tile(
+                [P, width, PACK], BF16, name="w_grouped", tag="w_grouped_%d" % width, align_bytes=64
+            )
+            engine_copy(
+                out=side_by_side[:].rearrange("p (c i) t -> p c t i", i=4),
+                in_=held[("w_raw", c)][:].rearrange("p t (c i) -> p c t i", i=4),
+            )
+            held[("w_grouped", c)] = side_by_side
 
-        def w_copy(q, on_scalar):
-            width = H1 if q < 4 else H2
-            wg = wgrp_pool.tile([P, width, 4], BF16, name="wg", tag="wg%d" % width, align_bytes=64)
-            dst = wg[:].rearrange("p (c i) t -> p c t i", i=4)
-            src = wraw[q][:].rearrange("p t (c i) -> p c t i", i=4)
-            if on_scalar:
-                nc.scalar.copy(out=dst, in_=src)
+        def quantise_weights(c):
+            values = held[("w_grouped", c)][:].rearrange("p h t -> p (h t)")
+            if c < L1_PASSES:
+                words, scales = w_l1_codes[:, c, :], w_l1_scales[:, c, :]
             else:
-                nc.vector.tensor_copy(out=dst, in_=src)
-            wgrp[q] = wg
+                words, scales = w_l2_codes[:, c - L1_PASSES, :], w_l2_scales[:, c - L1_PASSES, :]
+            nc.vector.quantize_mx(out=words.bitcast(FP8X4), scales=scales, in_=values)
 
-        def w_quant(q):
-            flat = wgrp[q][:].rearrange("p h t -> p (h t)")
-            if q < 4:
-                nc.vector.quantize_mx(out=wc1[:, q, :].bitcast(FP8X4), scales=ws1[:, q, :], in_=flat)
-            else:
-                nc.vector.quantize_mx(out=wc2[:, q - 4, :].bitcast(FP8X4), scales=ws2[:, q - 4, :], in_=flat)
 
-        def add_pairs(n):
-            ln = units[n][1]
-            s0 = sums.tile([P, ln, D], BF16, name="s0", tag="s0")
-            v = st[("nf1", n)][:].rearrange("p (j s k) -> p j s k", j=ln, s=2)
-            nc.vector.tensor_tensor(out=s0[:], in0=v[:, :, 0, :], in1=v[:, :, 1, :], op=ALU.add)
-            s1 = sums.tile([P, ln, H1], BF16, name="s1", tag="s1")
-            v = st[("a1", n)][:].rearrange("p (j s k) -> p j s k", j=ln, s=2)
-            nc.vector.tensor_tensor(out=s1[:], in0=v[:, :, 0, :], in1=v[:, :, 1, :], op=ALU.add)
-            st[("s0", n)] = s0
-            st[("s1", n)] = s1
+        def load_pair(n):
+            nf1_in = loads.tile([P, 4 * D], BF16, name="nf1_in", tag="nf1_in")
+            nc.sync.dma_start(out=nf1_in[:], in_=nf1_rows[:, 4 * D * n : 4 * D * (n + 1)])
+            a1_in = loads.tile([P, 4 * H1], BF16, name="a1_in", tag="a1_in")
+            nc.sync.dma_start(out=a1_in[:], in_=a1_rows[:, 4 * H1 * n : 4 * H1 * (n + 1)])
+            nf0_in = loads.tile([P, 2 * D], BF16, name="nf0_in", tag="nf0_in")
+            nc.sync.dma_start(out=nf0_in[:], in_=nf0_rows[:, 2 * D * n : 2 * D * (n + 1)])
+            held[("nf1", n)], held[("a1", n)], held[("nf0", n)] = nf1_in, a1_in, nf0_in
 
-        def transposes(n):
-            ln = units[n][1]
-            s0 = st[("s0", n)]
-            s1 = st[("s1", n)]
-            x32 = st[("nf0", n)][:].bitcast(F32)
-            for j in range(ln):
-                ta = psum.tile([P, 2, 4, P], BF16, name="ta%d" % j, tag="ta%d" % j)
+        def add_neighbours(n):
+            for kind, width in (("nf1", D), ("a1", H1)):
+                total = sums.tile([P, 2, width], BF16, name="sum_" + kind, tag="sum_" + kind)
+                rows = held[(kind, n)][:].rearrange("p (j s k) -> p j s k", j=2, s=2)
+                nc.vector.tensor_tensor(out=total[:], in0=rows[:, :, 0, :], in1=rows[:, :, 1, :], op=ALU.add)
+                held[("sum_" + kind, n)] = total
+
+        def transpose_pair(n):
+            for j in range(2):
+                agg0_t = psum.tile([P, 2, PACK, P], BF16, name="agg0_t%d" % j, tag="agg0_t%d" % j)
                 for g in range(2):
-                    for t in range(4):
-                        k0 = 512 * g + 128 * t
-                        nc.tensor.transpose(ta[:, g, t, :], s0[:, j, k0 : k0 + P], ident_b[:])
-                st[("ta", n, j)] = ta
-            tb = psum.tile([P, 2, 4, P], BF16, name="tb", tag="tb")
-            for j in range(ln):
-                for t in range(4):
-                    nc.tensor.transpose(tb[:, j, t, :], s1[:, j, 128 * t : 128 * (t + 1)], ident_b[:])
-            st[("tb", n)] = tb
-            for j in range(ln):
-                tn = psum.tile([P, 2, 2, P], F32, name="tn%d" % j, tag="tn%d" % j)
+                    for t in range(PACK):
+                        k0 = K_PASS * g + P * t
+                        nc.tensor.transpose(agg0_t[:, g, t, :], held[("sum_nf1", n)][:, j, k0 : k0 + P], identity_bf16[:])
+                held[("agg0_t", n, j)] = agg0_t
+            agg1_t = psum.tile([P, 2, PACK, P], BF16, name="agg1_t", tag="agg1_t")
+            for j in range(2):
+                for t in range(PACK):
+                    nc.tensor.transpose(agg1_t[:, j, t, :], held[("sum_a1", n)][:, j, P * t : P * (t + 1)], identity_bf16[:])
+            held[("agg1_t", n)] = agg1_t
+            nf0_words = held[("nf0", n)][:].bitcast(F32)
+            for j in range(2):
+                nf0_t = psum.tile([P, 2, 2, P], F32, name="nf0_t%d" % j, tag="nf0_t%d" % j)
                 for g in range(2):
                     for u in range(2):
-                        c0 = 512 * j + 256 * g + 128 * u
-                        nc.tensor.transpose(tn[:, g, u, :], x32[:, c0 : c0 + P], ident_f[:])
-                st[("tn", n, j)] = tn
+                        w0 = (D // 2) * j + (K_PASS // 2) * g + P * u
+                        nc.tensor.transpose(nf0_t[:, g, u, :], nf0_words[:, w0 : w0 + P], identity_f32[:])
+                held[("nf0_t", n, j)] = nf0_t
 
-        def evacuate(n):
-            ln = units[n][1]
-            gm = grp.tile([P, ln * 4 * P * 4], BF16, name="gm", tag="gm", align_bytes=64)
-            gm5 = gm[:].rearrange("p (q j b t) -> p j q b t", j=ln, q=4, b=P, t=4)
-            gm32 = gm[:].bitcast(F32).rearrange("p (q j b u) -> p j q b u", j=ln, q=4, b=P, u=2)
-            for j in range(ln):
+        def copy_out(n):
+            x_grouped = grouped.tile([P, L1_PASSES * PAIR * PACK], BF16, name="x_grouped", tag="x_grouped", align_bytes=64)
+            as_values = x_grouped[:].rearrange("p (c j b t) -> p j c b t", c=L1_PASSES, j=2, b=P, t=PACK)
+            as_words = x_grouped[:].bitcast(F32).rearrange("p (c j b u) -> p j c b u", c=L1_PASSES, j=2, b=P, u=2)
+            for j in range(2):
                 nc.scalar.activation(
-                    out=gm5[:, j, 2:4, :, :],
-                    in_=st[("ta", n, j)][:].rearrange("p g t b -> p g b t"),
+                    out=as_values[:, j, 2:4, :, :],
+                    in_=held[("agg0_t", n, j)][:].rearrange("p g t b -> p g b t"),
                     func=ACT.Copy,
                     scale=0.5,
                 )
-            g1 = grp.tile([P, ln * P * 4], BF16, name="g1", tag="g1", align_bytes=64)
+            agg1_grouped = grouped.tile([P, PAIR * PACK], BF16, name="agg1_grouped", tag="agg1_grouped", align_bytes=64)
             nc.scalar.activation(
-                out=g1[:].rearrange("p (j b t) -> p j b t", j=ln, b=P, t=4),
-                in_=st[("tb", n)][:, 0:ln, :, :].rearrange("p j t b -> p j b t"),
+                out=agg1_grouped[:].rearrange("p (j b t) -> p j b t", j=2, b=P, t=PACK),
+                in_=held[("agg1_t", n)][:].rearrange("p j t b -> p j b t"),
                 func=ACT.Copy,
                 scale=0.5,
             )
-            for j in range(ln):
+            for j in range(2):
                 nc.vector.tensor_copy(
-                    out=gm32[:, j, 0:2, :, :],
-                    in_=st[("tn", n, j)][:].rearrange("p g u b -> p g b u"),
+                    out=as_words[:, j, 0:2, :, :],
+                    in_=held[("nf0_t", n, j)][:].rearrange("p g u b -> p g b u"),
                 )
-            st[("gm", n)] = gm
-            st[("g1", n)] = g1
+            held[("x_grouped", n)], held[("agg1_grouped", n)] = x_grouped, agg1_grouped
 
-        def quantise(n):
-            ln = units[n][1]
-            gm = st[("gm", n)]
-            cm = cod.tile([P, ln * 4 * P], U32, name="cm", tag="cm", align_bytes=64)
-            sm = cod.tile([P, ln * 4 * P], U8, name="sm", tag="sm", align_bytes=64)
-            for h in range(2):
+        def quantise_pair(n):
+            x_codes = codes.tile([P, L1_PASSES * PAIR], U32, name="x_codes", tag="x_codes", align_bytes=64)
+            x_scales = codes.tile([P, L1_PASSES * PAIR], U8, name="x_scales", tag="x_scales", align_bytes=64)
+            for half in range(2):
+                cols = slice(2 * PAIR * half, 2 * PAIR * (half + 1))
                 nc.vector.quantize_mx(
-                    out=cm[:, 512 * h : 512 * (h + 1)].bitcast(FP8X4),
-                    scales=sm[:, 512 * h : 512 * (h + 1)],
-                    in_=gm[:, 2048 * h : 2048 * (h + 1)],
+                    out=x_codes[:, cols].bitcast(FP8X4),
+                    scales=x_scales[:, cols],
+                    in_=held[("x_grouped", n)][:, 2 * PAIR * PACK * half : 2 * PAIR * PACK * (half + 1)],
                 )
-            c1 = cod.tile([P, ln * P], U32, name="c1", tag="c1", align_bytes=64)
-            sc1 = cod.tile([P, ln * P], U8, name="sc1", tag="sc1", align_bytes=64)
-            nc.vector.quantize_mx(out=c1[:].bitcast(FP8X4), scales=sc1[:], in_=st[("g1", n)][:])
-            st[("cm", n)] = cm
-            st[("sm", n)] = sm
-            st[("c1", n)] = c1
-            st[("sc1", n)] = sc1
+            agg1_codes = codes.tile([P, PAIR], U32, name="agg1_codes", tag="agg1_codes", align_bytes=64)
+            agg1_scales = codes.tile([P, PAIR], U8, name="agg1_scales", tag="agg1_scales", align_bytes=64)
+            nc.vector.quantize_mx(out=agg1_codes[:].bitcast(FP8X4), scales=agg1_scales[:], in_=held[("agg1_grouped", n)][:])
+            held[("x_codes", n)], held[("x_scales", n)] = x_codes, x_scales
+            held[("agg1_codes", n)], held[("agg1_scales", n)] = agg1_codes, agg1_scales
+
 
         def layer1(n):
-            ln = units[n][1]
-            cm = st[("cm", n)]
-            sm = st[("sm", n)]
-            ga = grp.tile([P, ln * P * 4], BF16, name="ga", tag="ga", align_bytes=64)
-            gav = ga[:].rearrange("p (c h t) -> p h c t", c=2 * P, h=2, t=2)
+            x_codes, x_scales = held[("x_codes", n)], held[("x_scales", n)]
+            a0_grouped = grouped.tile([P, PAIR * PACK], BF16, name="a0_grouped", tag="a0_grouped", align_bytes=64)
+            by_bank = a0_grouped[:].rearrange("p (b h t) -> p h b t", b=PAIR, h=2, t=2)
             for h in range(2):
-                acc = psum.tile([P, 2, 2 * P], F32, name="acc%d" % h, tag="acc%d" % h)
+                a0_t = psum.tile([P, 2, PAIR], F32, name="a0_t%d" % h, tag="a0_t%d" % h)
                 for t in range(2):
-                    m0 = 128 * (2 * h + t)
-                    for q in range(4):
+                    hidden = slice(P * (2 * h + t), P * (2 * h + t + 1))
+                    for c in range(L1_PASSES):
+                        roots = slice(PAIR * c, PAIR * (c + 1))
                         nc.tensor.matmul_mx(
-                            out=acc[:, t, :],
-                            lhsT=wc1[:, q, m0 : m0 + P].bitcast(FP8X4),
-                            lhsT_scale=ws1[:, q, m0 : m0 + P],
-                            rhs=cm[:, 256 * q : 256 * (q + 1)].bitcast(FP8X4),
-                            rhs_scale=sm[:, 256 * q : 256 * (q + 1)],
-                            start=(q == 0),
-                            stop=(q == 3),
+                            out=a0_t[:, t, :],
+                            lhsT=w_l1_codes[:, c, hidden].bitcast(FP8X4),
+                            lhsT_scale=w_l1_scales[:, c, hidden],
+                            rhs=x_codes[:, roots].bitcast(FP8X4),
+                            rhs_scale=x_scales[:, roots],
+                            start=(c == 0),
+                            stop=(c == L1_PASSES - 1),
                         )
-                nc.scalar.activation(out=gav[:, h, :, :], in_=acc[:].rearrange("p t c -> p c t"), func=ACT.Relu)
-            st[("ga", n)] = ga
+                nc.scalar.activation(out=by_bank[:, h, :, :], in_=a0_t[:].rearrange("p t b -> p b t"), func=ACT.Relu)
+            held[("a0_grouped", n)] = a0_grouped
 
-        def quantise_a0(n):
-            ln = units[n][1]
-            ca = cod.tile([P, ln * P], U32, name="ca", tag="ca", align_bytes=64)
-            sa = cod.tile([P, ln * P], U8, name="sa", tag="sa", align_bytes=64)
-            nc.vector.quantize_mx(out=ca[:].bitcast(FP8X4), scales=sa[:], in_=st[("ga", n)][:])
-            st[("ca", n)] = ca
-            st[("sa", n)] = sa
+        def quantise_hidden(n):
+            a0_codes = codes.tile([P, PAIR], U32, name="a0_codes", tag="a0_codes", align_bytes=64)
+            a0_scales = codes.tile([P, PAIR], U8, name="a0_scales", tag="a0_scales", align_bytes=64)
+            nc.vector.quantize_mx(out=a0_codes[:].bitcast(FP8X4), scales=a0_scales[:], in_=held[("a0_grouped", n)][:])
+            held[("a0_codes", n)], held[("a0_scales", n)] = a0_codes, a0_scales
 
         def layer2(n):
-            x0, ln = units[n]
-            for j in range(ln):
-                x = x0 + j
-                if x % 4 == 0:
-                    ob_new = psum.tile([P, 4, P], F32, name="ob", tag="ob")
-                    st["ob"] = ob_new
-                ob = st["ob"]
-                cols = slice(128 * j, 128 * (j + 1))
-                nc.tensor.matmul_mx(
-                    out=ob[:, x % 4, :],
-                    lhsT=st[("ca", n)][:, cols].bitcast(FP8X4),
-                    lhsT_scale=st[("sa", n)][:, cols],
-                    rhs=wc2[:, 0, :].bitcast(FP8X4),
-                    rhs_scale=ws2[:, 0, :],
-                    start=True,
-                    stop=False,
-                )
-                nc.tensor.matmul_mx(
-                    out=ob[:, x % 4, :],
-                    lhsT=st[("c1", n)][:, cols].bitcast(FP8X4),
-                    lhsT_scale=st[("sc1", n)][:, cols],
-                    rhs=wc2[:, 1, :].bitcast(FP8X4),
-                    rhs_scale=ws2[:, 1, :],
-                    start=False,
-                    stop=True,
-                )
-                if x in store_end:
-                    first, length = store_end[x]
-                    ot = outp.tile([P, length, H2], F32, name="ot", tag="ot")
-                    nc.vector.tensor_relu(out=ot[:], in_=ob[:, first % 4 : first % 4 + length, :])
-                    nc.sync.dma_start(
-                        out=out_v[:, H2 * first : H2 * (first + length)], in_=ot[:].rearrange("p s c -> p (s c)")
+            for j in range(2):
+                x = 2 * n + j
+                place = x % SLICES_PER_BANK
+                if place == 0:
+                    held["out_bank"] = psum.tile([P, SLICES_PER_BANK, H2], F32, name="out_bank", tag="out_bank")
+                out_bank = held["out_bank"]
+                roots = slice(P * j, P * (j + 1))
+                for c, kind in enumerate(("a0", "agg1")):
+                    nc.tensor.matmul_mx(
+                        out=out_bank[:, place, :],
+                        lhsT=held[(kind + "_codes", n)][:, roots].bitcast(FP8X4),
+                        lhsT_scale=held[(kind + "_scales", n)][:, roots],
+                        rhs=w_l2_codes[:, c, :].bitcast(FP8X4),
+                        rhs_scale=w_l2_scales[:, c, :],
+                        start=(c == 0),
+                        stop=(c == 1),
                     )
+            count = 2 if n >= PAIRS - 2 else SLICES_PER_BANK
+            last = 2 * n + 1
+            if (last + 1) % count == 0:
+                first = last + 1 - count
+                result = results.tile([P, count, H2], F32, name="result", tag="result")
+                nc.vector.tensor_relu(
+                    out=result[:], in_=held["out_bank"][:, first % SLICES_PER_BANK : first % SLICES_PER_BANK + count, :]
+                )
+                nc.sync.dma_start(
+                    out=out_rows[:, H2 * first : H2 * (first + count)], in_=result[:].rearrange("p s c -> p (s c)")
+                )
 
-        load_weights_1()
-        load(0)
-        load(1)
-        load_weights_2()
-        for n in range(2, LA):
-            load(n)
-        w_copy(0, False)
-        w_copy(1, True)
-        w_quant(0)
-        w_copy(2, False)
-        w_copy(3, True)
-        w_quant(1)
-        w_quant(2)
-        add_pairs(0)
-        w_quant(3)
-        for i in range(nu + 2):
-            if i + LA < nu:
-                load(i + LA)
+
+        load_layer1_weights()
+        load_pair(0)
+        load_pair(1)
+        load_layer2_weights()
+        for n in range(2, AHEAD):
+            load_pair(n)
+
+        for c in range(L1_PASSES):
+            group_weights(c, nc.vector.tensor_copy if c % 2 == 0 else nc.scalar.copy)
+        for c in range(L1_PASSES - 1):
+            quantise_weights(c)
+        add_neighbours(0)
+        quantise_weights(L1_PASSES - 1)
+
+        for i in range(PAIRS + 2):
+            if i + AHEAD < PAIRS:
+                load_pair(i + AHEAD)
             if i >= 2:
-                quantise_a0(i - 2)
-            if i + 1 < nu:
-                add_pairs(i + 1)
-            if i < nu:
-                transposes(i)
-                evacuate(i)
-                quantise(i)
+                quantise_hidden(i - 2)
+            if i + 1 < PAIRS:
+                add_neighbours(i + 1)
+            if i < PAIRS:
+                transpose_pair(i)
+                copy_out(i)
+                quantise_pair(i)
             if i == 0:
-                w_copy(4, False)
-                w_copy(5, False)
-                w_quant(4)
-                w_quant(5)
-            if 1 <= i <= nu:
+                group_weights(4, nc.vector.tensor_copy)
+                group_weights(5, nc.vector.tensor_copy)
+                quantise_weights(4)
+                quantise_weights(5)
+            if 1 <= i <= PAIRS:
                 layer1(i - 1)
             if i >= 2:
                 layer2(i - 2)

@@ -34,7 +34,7 @@ def tile_graphsage_pb_t_kernel(tc, nf0, nf1, a1, w1_0, w2_0, w1_1, w2_1, out):
         sums = ctx.enter_context(tc.tile_pool(name="sums", bufs=3))
         grouped = ctx.enter_context(tc.tile_pool(name="grouped", bufs=2))
         codes = ctx.enter_context(tc.tile_pool(name="codes", bufs=3))
-        results = ctx.enter_context(tc.tile_pool(name="results", bufs=2))
+        results = ctx.enter_context(tc.tile_pool(name="results", bufs=4))
         psum = ctx.enter_context(tc.psum_pool(name="psum", bufs=1))
         ctx.enter_context(tc.manual_schedule())
 
@@ -45,8 +45,6 @@ def tile_graphsage_pb_t_kernel(tc, nf0, nf1, a1, w1_0, w2_0, w1_1, w2_1, out):
 
         identity_f32 = const.tile([P, P], F32, name="identity_f32")
         make_identity(nc, identity_f32[:])
-        identity_bf16 = const.tile([P, P], BF16, name="identity_bf16")
-        make_identity(nc, identity_bf16[:])
 
         w_l1_codes = const.tile([P, L1_PASSES, H1], U32, name="w_l1_codes", align_bytes=64)
         w_l1_scales = const.tile([P, L1_PASSES, H1], U8, name="w_l1_scales", align_bytes=64)
@@ -59,21 +57,24 @@ def tile_graphsage_pb_t_kernel(tc, nf0, nf1, a1, w1_0, w2_0, w1_1, w2_1, out):
         def load_layer1_weights():
             for c in range(L1_PASSES):
                 raw = weights_in.tile([P, PACK, H1], BF16, name="w_l1_raw", tag="w_l1_raw")
-                if c < 2:
-                    rows = w2_0[K_PASS * c : K_PASS * (c + 1), :]
-                    nc.sync.dma_start(
-                        out=raw[:].rearrange("p (u e) h -> p u e h", u=2, e=2),
-                        in_=rows.rearrange("(u p e) h -> p u e h", u=2, p=P, e=2),
-                    )
-                else:
-                    rows = w1_0[K_PASS * (c - 2) : K_PASS * (c - 1), :]
-                    nc.sync.dma_start(out=raw[:], in_=rows.rearrange("(t p) h -> p t h", t=PACK))
+                w = w2_0 if c < 2 else w1_0
+                rows = w[K_PASS * (c % 2) : K_PASS * (c % 2 + 1), :]
+                nc.sync.dma_start(
+                    out=raw[:].rearrange("p (u e) h -> p u e h", u=2, e=2),
+                    in_=rows.rearrange("(u p e) h -> p u e h", u=2, p=P, e=2),
+                )
                 held[("w_raw", c)] = raw
 
         def load_layer2_weights():
             for c, w in enumerate((w2_1, w1_1)):
                 raw = weights_in.tile([P, PACK, H2], BF16, name="w_l2_raw", tag="w_l2_raw", bufs=2)
-                nc.sync.dma_start(out=raw[:], in_=w.rearrange("(t p) c -> p t c", t=PACK))
+                if c == 0:
+                    nc.sync.dma_start(out=raw[:], in_=w.rearrange("(t p) c -> p t c", t=PACK))
+                else:
+                    nc.sync.dma_start(
+                        out=raw[:].rearrange("p (u e) c -> p u e c", u=2, e=2),
+                        in_=w.rearrange("(u p e) c -> p u e c", u=2, p=P, e=2),
+                    )
                 held[("w_raw", L1_PASSES + c)] = raw
 
         def group_weights(c, engine_copy):
@@ -106,24 +107,32 @@ def tile_graphsage_pb_t_kernel(tc, nf0, nf1, a1, w1_0, w2_0, w1_1, w2_1, out):
             held[("nf1", n)], held[("a1", n)], held[("nf0", n)] = nf1_in, a1_in, nf0_in
 
         def add_neighbours(n):
-            for kind, width in (("nf1", D), ("a1", H1)):
-                total = sums.tile([P, 2, width], BF16, name="sum_" + kind, tag="sum_" + kind)
+            mean = sums.tile([P, 2 * D + 2 * H1], BF16, name="mean", tag="mean")
+            for kind, width, start in (("nf1", D, 0), ("a1", H1, 2 * D)):
                 rows = held[(kind, n)][:].rearrange("p (j s k) -> p j s k", j=2, s=2)
-                nc.vector.tensor_tensor(out=total[:], in0=rows[:, :, 0, :], in1=rows[:, :, 1, :], op=ALU.add)
-                held[("sum_" + kind, n)] = total
+                nc.vector.tensor_tensor(
+                    out=mean[:, start : start + 2 * width].rearrange("p (j k) -> p j k", j=2),
+                    in0=rows[:, :, 0, :],
+                    in1=rows[:, :, 1, :],
+                    op=ALU.add,
+                )
+            nc.vector.tensor_scalar_mul(out=mean[:], in0=mean[:], scalar1=0.5)
+            held[("mean", n)] = mean
 
         def transpose_pair(n):
+            mean_words = held[("mean", n)][:].bitcast(F32)
             for j in range(2):
-                agg0_t = psum.tile([P, 2, PACK, P], BF16, name="agg0_t%d" % j, tag="agg0_t%d" % j)
+                agg0_t = psum.tile([P, 2, 2, P], F32, name="agg0_t%d" % j, tag="agg0_t%d" % j)
                 for g in range(2):
-                    for t in range(PACK):
-                        k0 = K_PASS * g + P * t
-                        nc.tensor.transpose(agg0_t[:, g, t, :], held[("sum_nf1", n)][:, j, k0 : k0 + P], identity_bf16[:])
+                    for u in range(2):
+                        w0 = (D // 2) * j + (K_PASS // 2) * g + P * u
+                        nc.tensor.transpose(agg0_t[:, g, u, :], mean_words[:, w0 : w0 + P], identity_f32[:])
                 held[("agg0_t", n, j)] = agg0_t
-            agg1_t = psum.tile([P, 2, PACK, P], BF16, name="agg1_t", tag="agg1_t")
+            agg1_t = psum.tile([P, 2, 2, P], F32, name="agg1_t", tag="agg1_t")
             for j in range(2):
-                for t in range(PACK):
-                    nc.tensor.transpose(agg1_t[:, j, t, :], held[("sum_a1", n)][:, j, P * t : P * (t + 1)], identity_bf16[:])
+                for u in range(2):
+                    w0 = D + (H1 // 2) * j + P * u
+                    nc.tensor.transpose(agg1_t[:, j, u, :], mean_words[:, w0 : w0 + P], identity_f32[:])
             held[("agg1_t", n)] = agg1_t
             nf0_words = held[("nf0", n)][:].bitcast(F32)
             for j in range(2):
@@ -136,24 +145,19 @@ def tile_graphsage_pb_t_kernel(tc, nf0, nf1, a1, w1_0, w2_0, w1_1, w2_1, out):
 
         def copy_out(n):
             x_grouped = grouped.tile([P, L1_PASSES * PAIR * PACK], BF16, name="x_grouped", tag="x_grouped", align_bytes=64)
-            as_values = x_grouped[:].rearrange("p (c j b t) -> p j c b t", c=L1_PASSES, j=2, b=P, t=PACK)
             as_words = x_grouped[:].bitcast(F32).rearrange("p (c j b u) -> p j c b u", c=L1_PASSES, j=2, b=P, u=2)
             for j in range(2):
-                nc.scalar.activation(
-                    out=as_values[:, j, 2:4, :, :],
-                    in_=held[("agg0_t", n, j)][:].rearrange("p g t b -> p g b t"),
-                    func=ACT.Copy,
-                    scale=0.5,
+                nc.scalar.copy(
+                    out=as_words[:, j, 2:4, :, :],
+                    in_=held[("agg0_t", n, j)][:].rearrange("p g u b -> p g b u"),
                 )
             agg1_grouped = grouped.tile([P, PAIR * PACK], BF16, name="agg1_grouped", tag="agg1_grouped", align_bytes=64)
-            nc.scalar.activation(
-                out=agg1_grouped[:].rearrange("p (j b t) -> p j b t", j=2, b=P, t=PACK),
-                in_=held[("agg1_t", n)][:].rearrange("p j t b -> p j b t"),
-                func=ACT.Copy,
-                scale=0.5,
+            nc.scalar.copy(
+                out=agg1_grouped[:].bitcast(F32).rearrange("p (j b u) -> p j b u", j=2, b=P, u=2),
+                in_=held[("agg1_t", n)][:].rearrange("p j u b -> p j b u"),
             )
             for j in range(2):
-                nc.vector.tensor_copy(
+                nc.scalar.copy(
                     out=as_words[:, j, 0:2, :, :],
                     in_=held[("nf0_t", n, j)][:].rearrange("p g u b -> p g b u"),
                 )
@@ -162,16 +166,19 @@ def tile_graphsage_pb_t_kernel(tc, nf0, nf1, a1, w1_0, w2_0, w1_1, w2_1, out):
         def quantise_pair(n):
             x_codes = codes.tile([P, L1_PASSES * PAIR], U32, name="x_codes", tag="x_codes", align_bytes=64)
             x_scales = codes.tile([P, L1_PASSES * PAIR], U8, name="x_scales", tag="x_scales", align_bytes=64)
-            for half in range(2):
+            agg1_codes = codes.tile([P, PAIR], U32, name="agg1_codes", tag="agg1_codes", align_bytes=64)
+            agg1_scales = codes.tile([P, PAIR], U8, name="agg1_scales", tag="agg1_scales", align_bytes=64)
+            for half in (1, 0):
                 cols = slice(2 * PAIR * half, 2 * PAIR * (half + 1))
                 nc.vector.quantize_mx(
                     out=x_codes[:, cols].bitcast(FP8X4),
                     scales=x_scales[:, cols],
                     in_=held[("x_grouped", n)][:, 2 * PAIR * PACK * half : 2 * PAIR * PACK * (half + 1)],
                 )
-            agg1_codes = codes.tile([P, PAIR], U32, name="agg1_codes", tag="agg1_codes", align_bytes=64)
-            agg1_scales = codes.tile([P, PAIR], U8, name="agg1_scales", tag="agg1_scales", align_bytes=64)
-            nc.vector.quantize_mx(out=agg1_codes[:].bitcast(FP8X4), scales=agg1_scales[:], in_=held[("agg1_grouped", n)][:])
+                if half == 1:
+                    nc.vector.quantize_mx(
+                        out=agg1_codes[:].bitcast(FP8X4), scales=agg1_scales[:], in_=held[("agg1_grouped", n)][:]
+                    )
             held[("x_codes", n)], held[("x_scales", n)] = x_codes, x_scales
             held[("agg1_codes", n)], held[("agg1_scales", n)] = agg1_codes, agg1_scales
 

from contextlib import ExitStack

import concourse.mybir as mybir
from concourse.masks import make_identity

F32 = mybir.dt.float32
BF16 = mybir.dt.bfloat16
U32 = mybir.dt.uint32
U8 = mybir.dt.uint8
FP8X4 = mybir.dt.float8_e4m3fn_x4
ACT = mybir.ActivationFunctionType
ALU = mybir.AluOpType

P = 128
PACK = 4
K_PASS = P * PACK
B, D, H1, H2 = 4096, 1024, 512, 128
FLOPS = 2 * B * (2 * D * H1 + 2 * H1 * H2)

PAIRS = B // (2 * P)
PAIR = 2 * P
L1_PASSES = 2 * D // K_PASS
AHEAD = 5
SLICES_PER_BANK = 4


def tile_graphsage_pb_t_kernel(tc, nf0, nf1, a1, w1_0, w2_0, w1_1, w2_1, out):
    nc = tc.nc
    with ExitStack() as ctx:
        const = ctx.enter_context(tc.tile_pool(name="const", bufs=1))
        weights_in = ctx.enter_context(tc.tile_pool(name="weights_in", bufs=L1_PASSES))
        weights_grouped = ctx.enter_context(tc.tile_pool(name="weights_grouped", bufs=L1_PASSES))
        loads = ctx.enter_context(tc.tile_pool(name="loads", bufs=AHEAD + 1))
        sums = ctx.enter_context(tc.tile_pool(name="sums", bufs=3))
        grouped = ctx.enter_context(tc.tile_pool(name="grouped", bufs=2))
        codes = ctx.enter_context(tc.tile_pool(name="codes", bufs=3))
        results = ctx.enter_context(tc.tile_pool(name="results", bufs=4))
        psum = ctx.enter_context(tc.psum_pool(name="psum", bufs=1))
        ctx.enter_context(tc.manual_schedule())

        nf0_rows = nf0.rearrange("(p x) k -> p (x k)", p=P)
        nf1_rows = nf1.rearrange("(p x) k -> p (x k)", p=P)
        a1_rows = a1.rearrange("(p x) k -> p (x k)", p=P)
        out_rows = out.rearrange("(p x) c -> p (x c)", p=P)

        identity_f32 = const.tile([P, P], F32, name="identity_f32")
        make_identity(nc, identity_f32[:])

        w_l1_codes = const.tile([P, L1_PASSES, H1], U32, name="w_l1_codes", align_bytes=64)
        w_l1_scales = const.tile([P, L1_PASSES, H1], U8, name="w_l1_scales", align_bytes=64)
        w_l2_codes = const.tile([P, 2, H2], U32, name="w_l2_codes", align_bytes=64)
        w_l2_scales = const.tile([P, 2, H2], U8, name="w_l2_scales", align_bytes=64)

        held = {}


        def load_layer1_weights():
            for c in range(L1_PASSES):
                raw = weights_in.tile([P, PACK, H1], BF16, name="w_l1_raw", tag="w_l1_raw")
                w = w2_0 if c < 2 else w1_0
                rows = w[K_PASS * (c % 2) : K_PASS * (c % 2 + 1), :]
                nc.sync.dma_start(
                    out=raw[:].rearrange("p (u e) h -> p u e h", u=2, e=2),
                    in_=rows.rearrange("(u p e) h -> p u e h", u=2, p=P, e=2),
                )
                held[("w_raw", c)] = raw

        def load_layer2_weights():
            for c, w in enumerate((w2_1, w1_1)):
                raw = weights_in.tile([P, PACK, H2], BF16, name="w_l2_raw", tag="w_l2_raw", bufs=2)
                if c == 0:
                    nc.sync.dma_start(out=raw[:], in_=w.rearrange("(t p) c -> p t c", t=PACK))
                else:
                    nc.sync.dma_start(
                        out=raw[:].rearrange("p (u e) c -> p u e c", u=2, e=2),
                        in_=w.rearrange("(u p e) c -> p u e c", u=2, p=P, e=2),
                    )
                held[("w_raw", L1_PASSES + c)] = raw

        def group_weights(c, engine_copy):
            width = H1 if c < L1_PASSES else H2
            side_by_side = weights_grouped.tile(
                [P, width, PACK], BF16, name="w_grouped", tag="w_grouped_%d" % width, align_bytes=64
            )
            engine_copy(
                out=side_by_side[:].rearrange("p (c i) t -> p c t i", i=4),
                in_=held[("w_raw", c)][:].rearrange("p t (c i) -> p c t i", i=4),
            )
            held[("w_grouped", c)] = side_by_side

        def quantise_weights(c):
            values = held[("w_grouped", c)][:].rearrange("p h t -> p (h t)")
            if c < L1_PASSES:
                words, scales = w_l1_codes[:, c, :], w_l1_scales[:, c, :]
            else:
                words, scales = w_l2_codes[:, c - L1_PASSES, :], w_l2_scales[:, c - L1_PASSES, :]
            nc.vector.quantize_mx(out=words.bitcast(FP8X4), scales=scales, in_=values)


        def load_pair(n):
            nf1_in = loads.tile([P, 4 * D], BF16, name="nf1_in", tag="nf1_in")
            nc.sync.dma_start(out=nf1_in[:], in_=nf1_rows[:, 4 * D * n : 4 * D * (n + 1)])
            a1_in = loads.tile([P, 4 * H1], BF16, name="a1_in", tag="a1_in")
            nc.sync.dma_start(out=a1_in[:], in_=a1_rows[:, 4 * H1 * n : 4 * H1 * (n + 1)])
            nf0_in = loads.tile([P, 2 * D], BF16, name="nf0_in", tag="nf0_in")
            nc.sync.dma_start(out=nf0_in[:], in_=nf0_rows[:, 2 * D * n : 2 * D * (n + 1)])
            held[("nf1", n)], held[("a1", n)], held[("nf0", n)] = nf1_in, a1_in, nf0_in

        def add_neighbours(n):
            mean = sums.tile([P, 2 * D + 2 * H1], BF16, name="mean", tag="mean")
            for kind, width, start in (("nf1", D, 0), ("a1", H1, 2 * D)):
                rows = held[(kind, n)][:].rearrange("p (j s k) -> p j s k", j=2, s=2)
                nc.vector.tensor_tensor(
                    out=mean[:, start : start + 2 * width].rearrange("p (j k) -> p j k", j=2),
                    in0=rows[:, :, 0, :],
                    in1=rows[:, :, 1, :],
                    op=ALU.add,
                )
            nc.vector.tensor_scalar_mul(out=mean[:], in0=mean[:], scalar1=0.5)
            held[("mean", n)] = mean

        def transpose_pair(n):
            mean_words = held[("mean", n)][:].bitcast(F32)
            for j in range(2):
                agg0_t = psum.tile([P, 2, 2, P], F32, name="agg0_t%d" % j, tag="agg0_t%d" % j)
                for g in range(2):
                    for u in range(2):
                        w0 = (D // 2) * j + (K_PASS // 2) * g + P * u
                        nc.tensor.transpose(agg0_t[:, g, u, :], mean_words[:, w0 : w0 + P], identity_f32[:])
                held[("agg0_t", n, j)] = agg0_t
            agg1_t = psum.tile([P, 2, 2, P], F32, name="agg1_t", tag="agg1_t")
            for j in range(2):
                for u in range(2):
                    w0 = D + (H1 // 2) * j + P * u
                    nc.tensor.transpose(agg1_t[:, j, u, :], mean_words[:, w0 : w0 + P], identity_f32[:])
            held[("agg1_t", n)] = agg1_t
            nf0_words = held[("nf0", n)][:].bitcast(F32)
            for j in range(2):
                nf0_t = psum.tile([P, 2, 2, P], F32, name="nf0_t%d" % j, tag="nf0_t%d" % j)
                for g in range(2):
                    for u in range(2):
                        w0 = (D // 2) * j + (K_PASS // 2) * g + P * u
                        nc.tensor.transpose(nf0_t[:, g, u, :], nf0_words[:, w0 : w0 + P], identity_f32[:])
                held[("nf0_t", n, j)] = nf0_t

        def copy_out(n):
            x_grouped = grouped.tile([P, L1_PASSES * PAIR * PACK], BF16, name="x_grouped", tag="x_grouped", align_bytes=64)
            as_words = x_grouped[:].bitcast(F32).rearrange("p (c j b u) -> p j c b u", c=L1_PASSES, j=2, b=P, u=2)
            for j in range(2):
                nc.scalar.copy(
                    out=as_words[:, j, 2:4, :, :],
                    in_=held[("agg0_t", n, j)][:].rearrange("p g u b -> p g b u"),
                )
            agg1_grouped = grouped.tile([P, PAIR * PACK], BF16, name="agg1_grouped", tag="agg1_grouped", align_bytes=64)
            nc.scalar.copy(
                out=agg1_grouped[:].bitcast(F32).rearrange("p (j b u) -> p j b u", j=2, b=P, u=2),
                in_=held[("agg1_t", n)][:].rearrange("p j u b -> p j b u"),
            )
            for j in range(2):
                nc.scalar.copy(
                    out=as_words[:, j, 0:2, :, :],
                    in_=held[("nf0_t", n, j)][:].rearrange("p g u b -> p g b u"),
                )
            held[("x_grouped", n)], held[("agg1_grouped", n)] = x_grouped, agg1_grouped

        def quantise_pair(n):
            x_codes = codes.tile([P, L1_PASSES * PAIR], U32, name="x_codes", tag="x_codes", align_bytes=64)
            x_scales = codes.tile([P, L1_PASSES * PAIR], U8, name="x_scales", tag="x_scales", align_bytes=64)
            agg1_codes = codes.tile([P, PAIR], U32, name="agg1_codes", tag="agg1_codes", align_bytes=64)
            agg1_scales = codes.tile([P, PAIR], U8, name="agg1_scales", tag="agg1_scales", align_bytes=64)
            for half in (1, 0):
                cols = slice(2 * PAIR * half, 2 * PAIR * (half + 1))
                nc.vector.quantize_mx(
                    out=x_codes[:, cols].bitcast(FP8X4),
                    scales=x_scales[:, cols],
                    in_=held[("x_grouped", n)][:, 2 * PAIR * PACK * half : 2 * PAIR * PACK * (half + 1)],
                )
                if half == 1:
                    nc.vector.quantize_mx(
                        out=agg1_codes[:].bitcast(FP8X4), scales=agg1_scales[:], in_=held[("agg1_grouped", n)][:]
                    )
            held[("x_codes", n)], held[("x_scales", n)] = x_codes, x_scales
            held[("agg1_codes", n)], held[("agg1_scales", n)] = agg1_codes, agg1_scales


        def layer1(n):
            x_codes, x_scales = held[("x_codes", n)], held[("x_scales", n)]
            a0_grouped = grouped.tile([P, PAIR * PACK], BF16, name="a0_grouped", tag="a0_grouped", align_bytes=64)
            by_bank = a0_grouped[:].rearrange("p (b h t) -> p h b t", b=PAIR, h=2, t=2)
            for h in range(2):
                a0_t = psum.tile([P, 2, PAIR], F32, name="a0_t%d" % h, tag="a0_t%d" % h)
                for t in range(2):
                    hidden = slice(P * (2 * h + t), P * (2 * h + t + 1))
                    for c in range(L1_PASSES):
                        roots = slice(PAIR * c, PAIR * (c + 1))
                        nc.tensor.matmul_mx(
                            out=a0_t[:, t, :],
                            lhsT=w_l1_codes[:, c, hidden].bitcast(FP8X4),
                            lhsT_scale=w_l1_scales[:, c, hidden],
                            rhs=x_codes[:, roots].bitcast(FP8X4),
                            rhs_scale=x_scales[:, roots],
                            start=(c == 0),
                            stop=(c == L1_PASSES - 1),
                        )
                nc.scalar.activation(out=by_bank[:, h, :, :], in_=a0_t[:].rearrange("p t b -> p b t"), func=ACT.Relu)
            held[("a0_grouped", n)] = a0_grouped

        def quantise_hidden(n):
            a0_codes = codes.tile([P, PAIR], U32, name="a0_codes", tag="a0_codes", align_bytes=64)
            a0_scales = codes.tile([P, PAIR], U8, name="a0_scales", tag="a0_scales", align_bytes=64)
            nc.vector.quantize_mx(out=a0_codes[:].bitcast(FP8X4), scales=a0_scales[:], in_=held[("a0_grouped", n)][:])
            held[("a0_codes", n)], held[("a0_scales", n)] = a0_codes, a0_scales

        def layer2(n):
            for j in range(2):
                x = 2 * n + j
                place = x % SLICES_PER_BANK
                if place == 0:
                    held["out_bank"] = psum.tile([P, SLICES_PER_BANK, H2], F32, name="out_bank", tag="out_bank")
                out_bank = held["out_bank"]
                roots = slice(P * j, P * (j + 1))
                for c, kind in enumerate(("a0", "agg1")):
                    nc.tensor.matmul_mx(
                        out=out_bank[:, place, :],
                        lhsT=held[(kind + "_codes", n)][:, roots].bitcast(FP8X4),
                        lhsT_scale=held[(kind + "_scales", n)][:, roots],
                        rhs=w_l2_codes[:, c, :].bitcast(FP8X4),
                        rhs_scale=w_l2_scales[:, c, :],
                        start=(c == 0),
                        stop=(c == 1),
                    )
            count = 2 if n >= PAIRS - 2 else SLICES_PER_BANK
            last = 2 * n + 1
            if (last + 1) % count == 0:
                first = last + 1 - count
                result = results.tile([P, count, H2], F32, name="result", tag="result")
                nc.vector.tensor_relu(
                    out=result[:], in_=held["out_bank"][:, first % SLICES_PER_BANK : first % SLICES_PER_BANK + count, :]
                )
                nc.sync.dma_start(
                    out=out_rows[:, H2 * first : H2 * (first + count)], in_=result[:].rearrange("p s c -> p (s c)")
                )


        load_layer1_weights()
        load_pair(0)
        load_pair(1)
        load_layer2_weights()
        for n in range(2, AHEAD):
            load_pair(n)

        for c in range(L1_PASSES):
            group_weights(c, nc.vector.tensor_copy if c % 2 == 0 else nc.scalar.copy)
        for c in range(L1_PASSES - 1):
            quantise_weights(c)
        add_neighbours(0)
        quantise_weights(L1_PASSES - 1)

        for i in range(PAIRS + 2):
            if i + AHEAD < PAIRS:
                load_pair(i + AHEAD)
            if i >= 2:
                quantise_hidden(i - 2)
            if i + 1 < PAIRS:
                add_neighbours(i + 1)
            if i < PAIRS:
                transpose_pair(i)
                copy_out(i)
                quantise_pair(i)
            if i == 0:
                group_weights(4, nc.vector.tensor_copy)
                group_weights(5, nc.vector.tensor_copy)
                quantise_weights(4)
                quantise_weights(5)
            if 1 <= i <= PAIRS:
                layer1(i - 1)
            if i >= 2:
                layer2(i - 2)
